import numpy as np
import ml_dtypes


def mxq(x, axis, fmt="e4m3"):
    dtype, down = {"e4m3": (ml_dtypes.float8_e4m3fn, 7), "e5m2": (ml_dtypes.float8_e5m2, 14)}[fmt]
    v = np.moveaxis(np.asarray(x, np.float32).astype(ml_dtypes.bfloat16).astype(np.float64), axis, -1)
    blocks = v.reshape(v.shape[:-1] + (-1, 32))
    amax = np.abs(blocks).max(-1, keepdims=True)
    byte = np.maximum(np.where(amax > 0, np.frexp(amax)[1] - 1 + 127, 0) - down, 1)
    scale = np.exp2(byte - 127.0)
    codes = (blocks / scale).astype(np.float32).astype(dtype).astype(np.float64)
    return np.moveaxis((codes * scale).reshape(v.shape), -1, axis)


WIDE = False


def mx_kscale(k):
    if not WIDE:
        return np.ones(k)
    levels = np.array([20, -20, 10, -10, 0])
    a = np.random.permutation(np.resize(levels, k // 512 * 4)).reshape(k // 512, 4)
    idx = np.arange(k)
    return np.exp2(a[idx // 512, idx % 128 // 32])


BF16 = ml_dtypes.bfloat16


def bf(x):
    return np.asarray(x, np.float32).astype(BF16)


def f64(x):
    return np.asarray(x).astype(np.float64)


B, D, OUT = 1536, 1024, 2048

TINY = 1e-15


def setup_inputs():
    s = mx_kscale(B)
    s = np.maximum(s, 1.0 / s)[:, None]
    x0 = bf(np.random.standard_normal((B, D)))
    z = bf(np.random.standard_normal((OUT, D)) * 0.5 / np.sqrt(D))
    r = bf(np.random.uniform(-1.0, 1.0, (OUT, 1)) * 4.0 / np.sqrt(D))
    bias = bf(np.random.standard_normal(OUT) * 0.1)
    g = bf(np.random.standard_normal((B, OUT)) * np.exp2(np.random.randint(-12, 1, (B, 1))) / s)
    xz = f64(x0) @ f64(z).T
    beta = np.sqrt(1.0 + np.sum(f64(x0) * f64(x0), axis=1, keepdims=True))
    return {"x": bf(f64(x0) * s), "z": z, "r": r, "bias": bias,
            "xz": np.asarray(xz, np.float32), "beta": np.asarray(beta, np.float32), "grad_out": g}


def reference(x, z, r, bias, xz, beta, grad_out):
    zf = f64(z)
    xzf = f64(xz)
    zn = np.sqrt(np.sum(zf * zf, axis=1))[None, :]
    sr = f64(r)[:, 0][None, :]
    c = np.cosh(sr)
    sh = np.sinh(sr)
    arg = c * xzf / zn - sh * f64(beta)
    a = np.arcsinh(arg)
    dv = f64(grad_out) * np.cosh(zn * a + f64(bias)[None, :])
    dxz = dv * c / np.sqrt(1.0 + arg * arg)
    t = np.sum(dv * a - dxz * xzf / zn, axis=0)
    m = mxq(dxz, 0, "e5m2").T @ mxq(f64(x), 0, "e4m3")
    return m + zf * (t / zn[0])[:, None]

@@ -1,0 +1,337 @@
+from contextlib import ExitStack
+
+import concourse.mybir as mybir
+from concourse.masks import make_identity
+
+F32 = mybir.dt.float32
+BF16 = mybir.dt.bfloat16
+U32 = mybir.dt.uint32
+U8 = mybir.dt.uint8
+E4M3_X4 = mybir.dt.float8_e4m3fn_x4
+E5M2_X4 = mybir.dt.float8_e5m2_x4
+ACT = mybir.ActivationFunctionType
+ALU = mybir.AluOpType
+
+TOKENS, D_MODEL, OUT_FEATURES = 1536, 1024, 2048
+FLOPS = 2 * TOKENS * D_MODEL * OUT_FEATURES
+
+P = 128
+PACK = 4
+K_PASS = P * PACK
+PASSES = TOKENS // K_PASS
+O_TILES = OUT_FEATURES // P
+BATCH = 2
+BATCHES = O_TILES // BATCH
+N_TILE = 512
+D_HALVES = D_MODEL // N_TILE
+G_BANK = 768
+BANKS_EMPTIED_BY_SCALAR = 2
+
+
+def tile_pvfc_v_kernel(tc, x, z, r, bias, xz, beta, grad_out, out):
+    nc = tc.nc
+
+    def pass_rows(matrix, g, first_col, width):
+        rows = matrix[g * K_PASS : (g + 1) * K_PASS, first_col : first_col + width]
+        return rows.rearrange("(q j) c -> q j c", j=PACK)
+
+    def load_token_rows(pool, matrix, dtype, first_col, width, name):
+        rows = pool.tile([P, PASSES, PACK, width], dtype, name=name, tag=name)
+        for g in range(PASSES):
+            nc.sync.dma_start(out=rows[:, g, :, :], in_=pass_rows(matrix, g, first_col, width))
+        return rows
+
+    with ExitStack() as stack:
+        stack.enter_context(tc.manual_schedule())
+        keep = stack.enter_context(tc.tile_pool(name="keep", bufs=1))
+        early = stack.enter_context(tc.tile_pool(name="early", bufs=2))
+        psum = stack.enter_context(tc.psum_pool(name="psum", bufs=4))
+
+        ident_f32 = keep.tile([P, P], F32)
+        make_identity(nc, ident_f32[:])
+        ident_bf16 = keep.tile([P, P], BF16)
+        make_identity(nc, ident_bf16[:])
+        one = keep.tile([P, 1], F32)
+        nc.vector.memset(one[:], 1.0)
+
+        xz_rows, y, log1p_sq, asinh, half_sign = {}, {}, {}, {}, {}
+
+        def xz_pass_to_o_layout(block):
+            bank = psum.tile([P, K_PASS], F32, name="xz_bank", tag="feed")
+            for j in range(PACK):
+                nc.tensor.transpose(bank[:, j * P : (j + 1) * P], block[:, j, :], ident_f32[:])
+            return bank
+
+        def shifted_xz(t):
+            batch, place = divmod(t, BATCH)
+            y[t] = early.tile([P, TOKENS], F32, name="y", tag="y")
+            for g in range(PASSES):
+                tokens = slice(g * K_PASS, (g + 1) * K_PASS)
+                bank = xz_pass_to_o_layout(xz_rows[batch][:, g, :, place * P : (place + 1) * P])
+                nc.vector.scalar_tensor_tensor(
+                    out=y[t][:, tokens], in0=beta_all[:, tokens], scalar=neg_kappa[:, t : t + 1],
+                    in1=bank[:], op0=ALU.mult, op1=ALU.add,
+                )
+            half_sign[t] = early.tile([P, TOKENS], BF16, name="half_sign", tag="half_sign", bufs=2 * BATCH)
+            nc.vector.tensor_scalar(
+                out=half_sign[t][:], in0=y[t][:], scalar1=0.0, scalar2=0.5, op0=ALU.is_ge, op1=ALU.subtract
+            )
+            if place == BATCH - 1 and batch + 2 < BATCHES:
+                xz_rows[batch + 2] = load_token_rows(early, xz, F32, (batch + 2) * BATCH * P, BATCH * P, "xz_rows")
+
+        with tc.tile_pool(name="setup", bufs=2) as setup:
+            vector_rows = setup.tile([P, P], BF16, bufs=1)
+            nc.vector.memset(vector_rows[:], 0.0)
+            nc.sync.dma_start(out=vector_rows[0:O_TILES, :], in_=r.rearrange("(t p) one -> t (p one)", p=P))
+            nc.sync.dma_start(out=vector_rows[O_TILES : 2 * O_TILES, :], in_=bias.rearrange("(t p) -> t p", p=P))
+            beta_rows = setup.tile([P, TOKENS], F32, bufs=1)
+            nc.sync.dma_start(out=beta_rows[:], in_=beta.rearrange("b one -> (b one)").partition_broadcast(P))
+            z_all = setup.tile([P, O_TILES, D_MODEL], BF16, bufs=1)
+            z_tiles = z.rearrange("(t p) d -> p t d", p=P)
+            quarter = O_TILES // 4
+            for first in (0, 2 * quarter, quarter, 3 * quarter):
+                nc.sync.dma_start(out=z_all[:, first : first + quarter, :], in_=z_tiles[:, first : first + quarter, :])
+            for batch in range(2):
+                xz_rows[batch] = load_token_rows(early, xz, F32, batch * BATCH * P, BATCH * P, "xz_rows")
+            x_raw = {}
+            for g in range(PASSES):
+                x_raw[g] = setup.tile([P, PACK, D_MODEL], BF16, name="x_raw", tag="x_raw", bufs=PASSES)
+                nc.sync.dma_start(out=x_raw[g][:], in_=pass_rows(x, g, 0, D_MODEL))
+
+            vector_cols = psum.tile([P, P], BF16, tag="feed")
+            nc.tensor.transpose(vector_cols[:], vector_rows[:], ident_bf16[:])
+            r_and_bias = keep.tile([P, 2 * O_TILES], F32)
+            nc.vector.tensor_copy(out=r_and_bias[:], in_=vector_cols[:, 0 : 2 * O_TILES])
+            r_col = r_and_bias[:, 0:O_TILES]
+            bias_col = r_and_bias[:, O_TILES : 2 * O_TILES]
+
+            beta_all = keep.tile([P, TOKENS], F32)
+            nc.vector.tensor_copy(
+                out=beta_all[:].rearrange("p (g j q) -> p g j q", g=PASSES, j=PACK),
+                in_=beta_rows[:].rearrange("p (g q j) -> p g j q", g=PASSES, j=PACK),
+            )
+
+            exp_r = keep.tile([P, O_TILES], F32)
+            nc.scalar.activation(out=exp_r[:], in_=r_col, func=ACT.Exp)
+            exp_neg_r = keep.tile([P, O_TILES], F32)
+            nc.scalar.activation(out=exp_neg_r[:], in_=r_col, func=ACT.Exp, scale=-1.0)
+            tanh_r = keep.tile([P, O_TILES], F32)
+            nc.scalar.activation(out=tanh_r[:], in_=r_col, func=ACT.Tanh)
+
+            zn_sq = keep.tile([P, O_TILES], F32)
+            for i in range(O_TILES // 2):
+                t = i
+                squares = setup.tile([P, D_MODEL], F32, name="squares_v", tag="squares_v")
+                nc.vector.scalar_tensor_tensor(
+                    out=squares[:], in0=z_all[:, t, :], scalar=1.0, in1=z_all[:, t, :],
+                    op0=ALU.mult, op1=ALU.mult, accum_out=zn_sq[:, t : t + 1],
+                )
+                t = O_TILES // 2 + i
+                squares = setup.tile([P, D_MODEL], BF16, name="squares_s", tag="squares_s")
+                nc.scalar.activation(out=squares[:], in_=z_all[:, t, :], func=ACT.Square, accum_out=zn_sq[:, t : t + 1])
+            zn = keep.tile([P, O_TILES], F32)
+            nc.scalar.activation(out=zn[:], in_=zn_sq[:], func=ACT.Sqrt)
+
+            neg_kappa = keep.tile([P, O_TILES], F32)
+            nc.vector.scalar_tensor_tensor(
+                out=neg_kappa[:], in0=zn[:], scalar=-1.0, in1=tanh_r[:], op0=ALU.mult, op1=ALU.mult
+            )
+            inv_zn = keep.tile([P, O_TILES], F32)
+            nc.vector.reciprocal(out=inv_zn[:], in_=zn[:])
+            two_cosh_r = keep.tile([P, O_TILES], F32)
+            nc.vector.tensor_tensor(out=two_cosh_r[:], in0=exp_r[:], in1=exp_neg_r[:], op=ALU.add)
+            cz = keep.tile([P, O_TILES], F32)
+            nc.vector.scalar_tensor_tensor(
+                out=cz[:], in0=two_cosh_r[:], scalar=0.5, in1=inv_zn[:], op0=ALU.mult, op1=ALU.mult
+            )
+            for t in range(BATCH):
+                shifted_xz(t)
+
+            two_zn = keep.tile([P, O_TILES], F32)
+            nc.vector.tensor_scalar_mul(out=two_zn[:], in0=zn[:], scalar1=2.0)
+            neg_two_zn = keep.tile([P, O_TILES], F32)
+            nc.vector.tensor_scalar_mul(out=neg_two_zn[:], in0=zn[:], scalar1=-2.0)
+            neg_bias = keep.tile([P, O_TILES], F32)
+            nc.vector.tensor_scalar_mul(out=neg_bias[:], in0=bias_col, scalar1=-1.0)
+            half_cosh_r = keep.tile([P, O_TILES], F32)
+            nc.vector.tensor_scalar_mul(out=half_cosh_r[:], in0=two_cosh_r[:], scalar1=0.25)
+            neg_inv_zn_sq = keep.tile([P, O_TILES], F32)
+            nc.vector.scalar_tensor_tensor(
+                out=neg_inv_zn_sq[:], in0=inv_zn[:], scalar=-1.0, in1=inv_zn[:], op0=ALU.mult, op1=ALU.mult
+            )
+
+            x_codes = keep.tile([P, PASSES, D_MODEL], U32, align_bytes=64)
+            x_scales = keep.tile([P, PASSES, D_MODEL], U8, align_bytes=64)
+            x_grouped = {}
+            for g in range(PASSES + 1):
+                if g < PASSES:
+                    x_grouped[g] = setup.tile([P, D_MODEL, PACK], BF16, name="x_grouped", tag="x_grouped", align_bytes=64)
+                    nc.vector.tensor_copy(out=x_grouped[g][:], in_=x_raw[g][:].rearrange("p j d -> p d j"))
+                if g > 0:
+                    nc.vector.quantize_mx(
+                        out=x_codes[:, g - 1, :].bitcast(E4M3_X4),
+                        scales=x_scales[:, g - 1, :],
+                        in_=x_grouped[g - 1][:].rearrange("p d j -> p (d j)"),
+                    )
+
+        late = stack.enter_context(tc.tile_pool(name="late", bufs=2, reuse_waits="tile"))
+        inv_root, exp_v, exp_neg_v, dxz, back_banks, dxz_codes, dxz_scales = {}, {}, {}, {}, {}, {}, {}
+        g_rows, xz_again, z_tile = {}, {}, {}
+        t_parts = keep.tile([P, O_TILES, 1 + PASSES], F32)
+        t_over_zn = keep.tile([P, O_TILES], F32)
+
+        def load_g_rows(batch):
+            if batch < BATCHES:
+                g_rows[batch] = load_token_rows(late, grad_out, BF16, batch * BATCH * P, BATCH * P, "g_rows")
+
+        def load_xz_again(t):
+            if t < O_TILES:
+                xz_again[t] = load_token_rows(late, xz, F32, t * P, P, "xz_again")
+
+        def load_z_tile(t):
+            if t < O_TILES:
+                z_tile[t] = late.tile([P, D_MODEL], BF16, name="z_tile", tag="z_tile")
+                nc.sync.dma_start(out=z_tile[t][:], in_=z[t * P : (t + 1) * P, :])
+
+        for first_two in range(2):
+            load_g_rows(first_two)
+            load_xz_again(first_two)
+            load_z_tile(first_two)
+
+        def first_log(t):
+            log1p_sq[t] = early.tile([P, TOKENS], F32, name="log1p_sq", tag="log1p_sq", bufs=2 * BATCH)
+            nc.scalar.activation(out=log1p_sq[t][:], in_=y[t][:], func=ACT.Square, scale=cz[:, t : t + 1])
+            asinh[t] = early.tile([P, TOKENS], F32, name="asinh", tag="asinh", bufs=3 * BATCH)
+            nc.scalar.activation(out=asinh[t][:], in_=y[t][:], func=ACT.Abs, scale=cz[:, t : t + 1])
+            nc.scalar.activation(out=log1p_sq[t][:], in_=log1p_sq[t][:], func=ACT.Ln, bias=one[:])
+
+        def root(t):
+            nc.scalar.activation(out=y[t][:], in_=log1p_sq[t][:], func=ACT.Exp, scale=0.5)
+            nc.vector.tensor_tensor(out=asinh[t][:], in0=asinh[t][:], in1=y[t][:], op=ALU.add)
+
+        def second_log(t):
+            nc.scalar.activation(out=asinh[t][:], in_=asinh[t][:], func=ACT.Ln)
+            nc.vector.tensor_tensor(out=asinh[t][:], in0=asinh[t][:], in1=half_sign[t][:], op=ALU.mult)
+
+        def exponentials(t):
+            inv_root[t] = late.tile([P, TOKENS], F32, name="inv_root", tag="inv_root")
+            nc.scalar.activation(out=inv_root[t][:], in_=log1p_sq[t][:], func=ACT.Exp, scale=-0.5)
+            exp_v[t] = late.tile([P, TOKENS], F32, name="exp_v", tag="exp_v")
+            nc.scalar.activation(
+                out=exp_v[t][:], in_=asinh[t][:], func=ACT.Exp, scale=two_zn[:, t : t + 1], bias=bias_col[:, t : t + 1]
+            )
+            exp_neg_v[t] = late.tile([P, TOKENS], F32, name="exp_neg_v", tag="exp_neg_v")
+            nc.scalar.activation(
+                out=exp_neg_v[t][:], in_=asinh[t][:], func=ACT.Exp,
+                scale=neg_two_zn[:, t : t + 1], bias=neg_bias[:, t : t + 1],
+            )
+
+        def grad_v(t):
+            batch, place = divmod(t, BATCH)
+            nc.vector.tensor_tensor(out=exp_v[t][:], in0=exp_v[t][:], in1=exp_neg_v[t][:], op=ALU.add)
+            blocks = G_BANK // P
+            for h in range(TOKENS // G_BANK):
+                bank = psum.tile([P, G_BANK], BF16, name="g_bank", tag="feed")
+                for i in range(blocks):
+                    g, j = divmod(h * blocks + i, PACK)
+                    nc.tensor.transpose(
+                        bank[:, i * P : (i + 1) * P], g_rows[batch][:, g, j, place * P : (place + 1) * P], ident_bf16[:]
+                    )
+                tokens = slice(h * G_BANK, (h + 1) * G_BANK)
+                nc.vector.tensor_tensor(out=exp_neg_v[t][:, tokens], in0=bank[:], in1=exp_v[t][:, tokens], op=ALU.mult)
+            if place == BATCH - 1:
+                load_g_rows(batch + 2)
+
+        def grad_xz(t):
+            dv2 = exp_neg_v[t]
+            dxz[t] = late.tile([P, TOKENS], F32, name="dxz", tag="dxz")
+            nc.vector.scalar_tensor_tensor(
+                out=dxz[t][:], in0=dv2[:], scalar=half_cosh_r[:, t : t + 1], in1=inv_root[t][:],
+                op0=ALU.mult, op1=ALU.mult,
+            )
+            nc.vector.scalar_tensor_tensor(
+                out=exp_v[t][:], in0=dv2[:], scalar=inv_zn[:, t : t + 1], in1=asinh[t][:],
+                op0=ALU.mult, op1=ALU.mult, accum_out=t_parts[:, t, 0:1],
+            )
+            for g in range(PASSES):
+                tokens = slice(g * K_PASS, (g + 1) * K_PASS)
+                bank = xz_pass_to_o_layout(xz_again[t][:, g, :, :])
+                nc.vector.scalar_tensor_tensor(
+                    out=dv2[:, tokens], in0=dxz[t][:, tokens], scalar=neg_inv_zn_sq[:, t : t + 1], in1=bank[:],
+                    op0=ALU.mult, op1=ALU.mult, accum_out=t_parts[:, t, 1 + g : 2 + g],
+                )
+            load_xz_again(t + 2)
+            back_banks[t] = []
+            for g in range(PASSES):
+                bank = psum.tile([P, K_PASS], F32, name="back_bank", tag="back")
+                for j in range(PACK):
+                    first = (g * PACK + j) * P
+                    nc.tensor.transpose(bank[:, j * P : (j + 1) * P], dxz[t][:, first : first + P], ident_f32[:])
+                back_banks[t].append(bank)
+
+        def quantise_dxz(t):
+            grouped = late.tile([P, PASSES, P, PACK], BF16, name="dxz_grouped", tag="dxz_grouped", align_bytes=64)
+            for g in range(PASSES):
+                by_feature = back_banks[t][g][:].rearrange("p (j o) -> p o j", j=PACK)
+                if g < BANKS_EMPTIED_BY_SCALAR:
+                    nc.scalar.copy(out=grouped[:, g, :, :], in_=by_feature)
+                else:
+                    nc.vector.tensor_copy(out=grouped[:, g, :, :], in_=by_feature)
+            dxz_codes[t] = late.tile([P, PASSES, P], U32, name="dxz_codes", tag="dxz_codes", align_bytes=64)
+            dxz_scales[t] = late.tile([P, PASSES, P], U8, name="dxz_scales", tag="dxz_scales", align_bytes=64)
+            for g in range(PASSES):
+                nc.vector.quantize_mx(
+                    out=dxz_codes[t][:, g, :].bitcast(E5M2_X4),
+                    scales=dxz_scales[t][:, g, :],
+                    in_=grouped[:, g, :, :].rearrange("p o j -> p (o j)"),
+                )
+
+        def finish(t):
+            nc.vector.tensor_reduce(
+                out=t_over_zn[:, t : t + 1], in_=t_parts[:, t, :], axis=mybir.AxisListType.X, op=ALU.add
+            )
+            result = late.tile([P, D_MODEL], F32, name="result", tag="result")
+            for half in range(D_HALVES):
+                cols = slice(half * N_TILE, (half + 1) * N_TILE)
+                product = psum.tile([P, N_TILE], F32, name="product", tag="back")
+                for g in range(PASSES):
+                    nc.tensor.matmul_mx(
+                        out=product[:],
+                        lhsT=dxz_codes[t][:, g, :].bitcast(E5M2_X4),
+                        lhsT_scale=dxz_scales[t][:, g, :],
+                        rhs=x_codes[:, g, cols].bitcast(E4M3_X4),
+                        rhs_scale=x_scales[:, g, cols],
+                        start=(g == 0),
+                        stop=(g == PASSES - 1),
+                    )
+                nc.vector.scalar_tensor_tensor(
+                    out=result[:, cols], in0=z_tile[t][:, cols], scalar=t_over_zn[:, t : t + 1], in1=product[:],
+                    op0=ALU.mult, op1=ALU.add,
+                )
+            nc.sync.dma_start(out=out[t * P : (t + 1) * P, :], in_=result[:])
+            load_z_tile(t + 2)
+
+        def run(stage, t):
+            if 0 <= t < O_TILES:
+                stage(t)
+
+        for k in range(-1, BATCHES + 2):
+            t = BATCH * k
+            run(grad_v, t - 2)
+            run(finish, t - 3)
+            run(grad_xz, t - 2)
+            run(second_log, t)
+            run(second_log, t + 1)
+            run(first_log, t + 2)
+            run(quantise_dxz, t - 2)
+            run(first_log, t + 3)
+            run(grad_v, t - 1)
+            run(finish, t - 2)
+            run(grad_xz, t - 1)
+            run(root, t + 2)
+            run(root, t + 3)
+            run(exponentials, t)
+            run(quantise_dxz, t - 1)
+            run(exponentials, t + 1)
+            run(shifted_xz, t + 4)
+            run(shifted_xz, t + 5)

@@ -24,8 +24,7 @@ BATCH = 2
 BATCHES = O_TILES // BATCH
 N_TILE = 512
 D_HALVES = D_MODEL // N_TILE
-G_BANK = 768
-BANKS_EMPTIED_BY_SCALAR = 2
+BANKS_EMPTIED_BY_SCALAR = 1
 
 
 def tile_pvfc_v_kernel(tc, x, z, r, bias, xz, beta, grad_out, out):
@@ -76,6 +75,8 @@ def tile_pvfc_v_kernel(tc, x, z, r, bias, xz, beta, grad_out, out):
             nc.vector.tensor_scalar(
                 out=half_sign[t][:], in0=y[t][:], scalar1=0.0, scalar2=0.5, op0=ALU.is_ge, op1=ALU.subtract
             )
+            log1p_sq[t] = early.tile([P, TOKENS], F32, name="log1p_sq", tag="log1p_sq", bufs=2 * BATCH)
+            nc.gpsimd.tensor_tensor(out=log1p_sq[t][:], in0=y[t][:], in1=y[t][:], op=ALU.mult)
             if place == BATCH - 1 and batch + 2 < BATCHES:
                 xz_rows[batch + 2] = load_token_rows(early, xz, F32, (batch + 2) * BATCH * P, BATCH * P, "xz_rows")
 
@@ -144,6 +145,8 @@ def tile_pvfc_v_kernel(tc, x, z, r, bias, xz, beta, grad_out, out):
             nc.vector.scalar_tensor_tensor(
                 out=cz[:], in0=two_cosh_r[:], scalar=0.5, in1=inv_zn[:], op0=ALU.mult, op1=ALU.mult
             )
+            cz_sq = keep.tile([P, O_TILES], F32)
+            nc.vector.tensor_tensor(out=cz_sq[:], in0=cz[:], in1=cz[:], op=ALU.mult)
             for t in range(BATCH):
                 shifted_xz(t)
 
@@ -176,8 +179,8 @@ def tile_pvfc_v_kernel(tc, x, z, r, bias, xz, beta, grad_out, out):
 
         late = stack.enter_context(tc.tile_pool(name="late", bufs=2, reuse_waits="tile"))
         inv_root, exp_v, exp_neg_v, dxz, back_banks, dxz_codes, dxz_scales = {}, {}, {}, {}, {}, {}, {}
-        g_rows, xz_again, z_tile = {}, {}, {}
-        t_parts = keep.tile([P, O_TILES, 1 + PASSES], F32)
+        g_rows, xz_again, z_tile, dv2_rows = {}, {}, {}, {}
+        t_parts = keep.tile([P, O_TILES, 2 * PASSES], F32)
         t_over_zn = keep.tile([P, O_TILES], F32)
 
         def load_g_rows(batch):
@@ -199,19 +202,17 @@ def tile_pvfc_v_kernel(tc, x, z, r, bias, xz, beta, grad_out, out):
             load_z_tile(first_two)
 
         def first_log(t):
-            log1p_sq[t] = early.tile([P, TOKENS], F32, name="log1p_sq", tag="log1p_sq", bufs=2 * BATCH)
-            nc.scalar.activation(out=log1p_sq[t][:], in_=y[t][:], func=ACT.Square, scale=cz[:, t : t + 1])
             asinh[t] = early.tile([P, TOKENS], F32, name="asinh", tag="asinh", bufs=3 * BATCH)
             nc.scalar.activation(out=asinh[t][:], in_=y[t][:], func=ACT.Abs, scale=cz[:, t : t + 1])
-            nc.scalar.activation(out=log1p_sq[t][:], in_=log1p_sq[t][:], func=ACT.Ln, bias=one[:])
+            nc.scalar.activation(out=log1p_sq[t][:], in_=log1p_sq[t][:], func=ACT.Ln, scale=cz_sq[:, t : t + 1], bias=one[:])
 
         def root(t):
             nc.scalar.activation(out=y[t][:], in_=log1p_sq[t][:], func=ACT.Exp, scale=0.5)
-            nc.vector.tensor_tensor(out=asinh[t][:], in0=asinh[t][:], in1=y[t][:], op=ALU.add)
+            nc.gpsimd.tensor_tensor(out=asinh[t][:], in0=asinh[t][:], in1=y[t][:], op=ALU.add)
 
         def second_log(t):
             nc.scalar.activation(out=asinh[t][:], in_=asinh[t][:], func=ACT.Ln)
-            nc.vector.tensor_tensor(out=asinh[t][:], in0=asinh[t][:], in1=half_sign[t][:], op=ALU.mult)
+            nc.gpsimd.tensor_tensor(out=asinh[t][:], in0=asinh[t][:], in1=half_sign[t][:], op=ALU.mult)
 
         def exponentials(t):
             inv_root[t] = late.tile([P, TOKENS], F32, name="inv_root", tag="inv_root")
@@ -228,37 +229,47 @@ def tile_pvfc_v_kernel(tc, x, z, r, bias, xz, beta, grad_out, out):
 
         def grad_v(t):
             batch, place = divmod(t, BATCH)
-            nc.vector.tensor_tensor(out=exp_v[t][:], in0=exp_v[t][:], in1=exp_neg_v[t][:], op=ALU.add)
-            blocks = G_BANK // P
-            for h in range(TOKENS // G_BANK):
-                bank = psum.tile([P, G_BANK], BF16, name="g_bank", tag="feed")
-                for i in range(blocks):
-                    g, j = divmod(h * blocks + i, PACK)
-                    nc.tensor.transpose(
-                        bank[:, i * P : (i + 1) * P], g_rows[batch][:, g, j, place * P : (place + 1) * P], ident_bf16[:]
+            dv2_rows[t] = late.tile([P, PASSES, PACK, P], F32, name="dv2_rows", tag="dv2_rows")
+            for g in range(PASSES):
+                bank = psum.tile([P, K_PASS], F32, name="cosh_bank", tag="feed")
+                for j in range(PACK):
+                    block = slice((g * PACK + j) * P, (g * PACK + j + 1) * P)
+                    nc.tensor.matmul(
+                        out=bank[:, j * P : (j + 1) * P], lhsT=exp_v[t][:, block], rhs=ident_f32[:],
+                        is_transpose=True, start=True, stop=False,
                     )
-                tokens = slice(h * G_BANK, (h + 1) * G_BANK)
-                nc.vector.tensor_tensor(out=exp_neg_v[t][:, tokens], in0=bank[:], in1=exp_v[t][:, tokens], op=ALU.mult)
+                    nc.tensor.matmul(
+                        out=bank[:, j * P : (j + 1) * P], lhsT=exp_neg_v[t][:, block], rhs=ident_f32[:],
+                        is_transpose=True, start=False, stop=True,
+                    )
+                nc.vector.tensor_tensor(
+                    out=dv2_rows[t][:, g, :, :], in0=g_rows[batch][:, g, :, place * P : (place + 1) * P],
+                    in1=bank[:].rearrange("p (j o) -> p j o", j=PACK), op=ALU.mult,
+                )
             if place == BATCH - 1:
                 load_g_rows(batch + 2)
 
         def grad_xz(t):
-            dv2 = exp_neg_v[t]
             dxz[t] = late.tile([P, TOKENS], F32, name="dxz", tag="dxz")
-            nc.vector.scalar_tensor_tensor(
-                out=dxz[t][:], in0=dv2[:], scalar=half_cosh_r[:, t : t + 1], in1=inv_root[t][:],
-                op0=ALU.mult, op1=ALU.mult,
-            )
-            nc.vector.scalar_tensor_tensor(
-                out=exp_v[t][:], in0=dv2[:], scalar=inv_zn[:, t : t + 1], in1=asinh[t][:],
-                op0=ALU.mult, op1=ALU.mult, accum_out=t_parts[:, t, 0:1],
-            )
+            for g in range(PASSES):
+                tokens = slice(g * K_PASS, (g + 1) * K_PASS)
+                bank = psum.tile([P, K_PASS], F32, name="dv2_bank", tag="feed")
+                for j in range(PACK):
+                    nc.tensor.transpose(bank[:, j * P : (j + 1) * P], dv2_rows[t][:, g, j, :], ident_f32[:])
+                nc.vector.scalar_tensor_tensor(
+                    out=dxz[t][:, tokens], in0=bank[:], scalar=half_cosh_r[:, t : t + 1], in1=inv_root[t][:, tokens],
+                    op0=ALU.mult, op1=ALU.mult,
+                )
+                nc.vector.scalar_tensor_tensor(
+                    out=exp_v[t][:, tokens], in0=bank[:], scalar=inv_zn[:, t : t + 1], in1=asinh[t][:, tokens],
+                    op0=ALU.mult, op1=ALU.mult, accum_out=t_parts[:, t, g : g + 1],
+                )
             for g in range(PASSES):
                 tokens = slice(g * K_PASS, (g + 1) * K_PASS)
                 bank = xz_pass_to_o_layout(xz_again[t][:, g, :, :])
                 nc.vector.scalar_tensor_tensor(
-                    out=dv2[:, tokens], in0=dxz[t][:, tokens], scalar=neg_inv_zn_sq[:, t : t + 1], in1=bank[:],
-                    op0=ALU.mult, op1=ALU.mult, accum_out=t_parts[:, t, 1 + g : 2 + g],
+                    out=exp_neg_v[t][:, tokens], in0=dxz[t][:, tokens], scalar=neg_inv_zn_sq[:, t : t + 1], in1=bank[:],
+                    op0=ALU.mult, op1=ALU.mult, accum_out=t_parts[:, t, PASSES + g : PASSES + g + 1],
                 )
             load_xz_again(t + 2)
             back_banks[t] = []

@@ -24,7 +24,7 @@ BATCH = 2
 BATCHES = O_TILES // BATCH
 N_TILE = 512
 D_HALVES = D_MODEL // N_TILE
-BANKS_EMPTIED_BY_SCALAR = 1
+BANKS_EMPTIED_BY_SCALAR = 2
 
 
 def tile_pvfc_v_kernel(tc, x, z, r, bias, xz, beta, grad_out, out):

@@ -24,7 +24,7 @@ BATCH = 2
 BATCHES = O_TILES // BATCH
 N_TILE = 512
 D_HALVES = D_MODEL // N_TILE
-BANKS_EMPTIED_BY_SCALAR = 2
+BANKS_EMPTIED_BY_SCALAR = 1
 
 
 def tile_pvfc_v_kernel(tc, x, z, r, bias, xz, beta, grad_out, out):
@@ -85,13 +85,13 @@ def tile_pvfc_v_kernel(tc, x, z, r, bias, xz, beta, grad_out, out):
             nc.vector.memset(vector_rows[:], 0.0)
             nc.sync.dma_start(out=vector_rows[0:O_TILES, :], in_=r.rearrange("(t p) one -> t (p one)", p=P))
             nc.sync.dma_start(out=vector_rows[O_TILES : 2 * O_TILES, :], in_=bias.rearrange("(t p) -> t p", p=P))
-            beta_rows = setup.tile([P, TOKENS], F32, bufs=1)
-            nc.sync.dma_start(out=beta_rows[:], in_=beta.rearrange("b one -> (b one)").partition_broadcast(P))
             z_all = setup.tile([P, O_TILES, D_MODEL], BF16, bufs=1)
             z_tiles = z.rearrange("(t p) d -> p t d", p=P)
             quarter = O_TILES // 4
             for first in (0, 2 * quarter, quarter, 3 * quarter):
                 nc.sync.dma_start(out=z_all[:, first : first + quarter, :], in_=z_tiles[:, first : first + quarter, :])
+            beta_rows = setup.tile([P, TOKENS], F32, bufs=1)
+            nc.sync.dma_start(out=beta_rows[:], in_=beta.rearrange("b one -> (b one)").partition_broadcast(P))
             for batch in range(2):
                 xz_rows[batch] = load_token_rows(early, xz, F32, batch * BATCH * P, BATCH * P, "xz_rows")
             x_raw = {}
@@ -105,12 +105,6 @@ def tile_pvfc_v_kernel(tc, x, z, r, bias, xz, beta, grad_out, out):
             nc.vector.tensor_copy(out=r_and_bias[:], in_=vector_cols[:, 0 : 2 * O_TILES])
             r_col = r_and_bias[:, 0:O_TILES]
             bias_col = r_and_bias[:, O_TILES : 2 * O_TILES]
-
-            beta_all = keep.tile([P, TOKENS], F32)
-            nc.vector.tensor_copy(
-                out=beta_all[:].rearrange("p (g j q) -> p g j q", g=PASSES, j=PACK),
-                in_=beta_rows[:].rearrange("p (g q j) -> p g j q", g=PASSES, j=PACK),
-            )
 
             exp_r = keep.tile([P, O_TILES], F32)
             nc.scalar.activation(out=exp_r[:], in_=r_col, func=ACT.Exp)
@@ -132,6 +126,12 @@ def tile_pvfc_v_kernel(tc, x, z, r, bias, xz, beta, grad_out, out):
                 nc.scalar.activation(out=squares[:], in_=z_all[:, t, :], func=ACT.Square, accum_out=zn_sq[:, t : t + 1])
             zn = keep.tile([P, O_TILES], F32)
             nc.scalar.activation(out=zn[:], in_=zn_sq[:], func=ACT.Sqrt)
+
+            beta_all = keep.tile([P, TOKENS], F32)
+            nc.vector.tensor_copy(
+                out=beta_all[:].rearrange("p (g j q) -> p g j q", g=PASSES, j=PACK),
+                in_=beta_rows[:].rearrange("p (g q j) -> p g j q", g=PASSES, j=PACK),
+            )
 
             neg_kappa = keep.tile([P, O_TILES], F32)
             nc.vector.scalar_tensor_tensor(
@@ -319,7 +319,7 @@ def tile_pvfc_v_kernel(tc, x, z, r, bias, xz, beta, grad_out, out):
                     out=result[:, cols], in0=z_tile[t][:, cols], scalar=t_over_zn[:, t : t + 1], in1=product[:],
                     op0=ALU.mult, op1=ALU.add,
                 )
-            nc.sync.dma_start(out=out[t * P : (t + 1) * P, :], in_=result[:])
+                nc.sync.dma_start(out=out[t * P : (t + 1) * P, cols], in_=result[:, cols])
             load_z_tile(t + 2)
 
         def run(stage, t):

@@ -52,6 +52,8 @@ def tile_pvfc_v_kernel(tc, x, z, r, bias, xz, beta, grad_out, out):
         make_identity(nc, ident_bf16[:])
         one = keep.tile([P, 1], F32)
         nc.vector.memset(one[:], 1.0)
+        half_exponent = keep.tile([P, O_TILES], F32)
+        nc.vector.memset(half_exponent[:], 0.5)
 
         xz_rows, y, log1p_sq, asinh, half_sign = {}, {}, {}, {}, {}
 
@@ -76,24 +78,63 @@ def tile_pvfc_v_kernel(tc, x, z, r, bias, xz, beta, grad_out, out):
                 out=half_sign[t][:], in0=y[t][:], scalar1=0.0, scalar2=0.5, op0=ALU.is_ge, op1=ALU.subtract
             )
             log1p_sq[t] = early.tile([P, TOKENS], F32, name="log1p_sq", tag="log1p_sq", bufs=2 * BATCH)
-            nc.gpsimd.tensor_tensor(out=log1p_sq[t][:], in0=y[t][:], in1=y[t][:], op=ALU.mult)
+            if t < BATCH:
+                nc.scalar.activation(out=log1p_sq[t][:], in_=y[t][:], func=ACT.Square)
+            else:
+                nc.gpsimd.tensor_tensor(out=log1p_sq[t][:], in0=y[t][:], in1=y[t][:], op=ALU.mult)
             if place == BATCH - 1 and batch + 2 < BATCHES:
                 xz_rows[batch + 2] = load_token_rows(early, xz, F32, (batch + 2) * BATCH * P, BATCH * P, "xz_rows")
+
+        def half_abs_by_gpsimd(t):
+            return t >= BATCH and t % 2 == 1
+
+        def half_abs(t):
+            asinh[t] = early.tile([P, TOKENS], F32, name="asinh", tag="asinh", bufs=3 * BATCH)
+            if half_abs_by_gpsimd(t):
+                nc.gpsimd.tensor_tensor(out=asinh[t][:], in0=y[t][:], in1=half_sign[t][:], op=ALU.mult)
+            else:
+                nc.scalar.activation(out=asinh[t][:], in_=y[t][:], func=ACT.Abs, scale=0.5)
+
+        def first_log(t):
+            half_abs(t)
+            nc.scalar.activation(out=log1p_sq[t][:], in_=log1p_sq[t][:], func=ACT.Ln, scale=cz_sq[:, t : t + 1], bias=one[:])
+
+        def root(t):
+            nc.scalar.activation(
+                out=y[t][:], in_=log1p_sq[t][:], func=ACT.Exp, scale=0.5, bias=neg_ln_two_cz[:, t : t + 1]
+            )
+            nc.gpsimd.tensor_tensor(out=asinh[t][:], in0=asinh[t][:], in1=y[t][:], op=ALU.add)
+
+        zn_sq, zn, inv_zn, neg_kappa, two_cz, inv_two_cz, neg_ln_two_cz, cz_sq, two_zn, neg_two_zn, neg_inv_zn_sq = [
+            keep.tile([P, O_TILES], F32, name=name, tag=name)
+            for name in (
+                "zn_sq", "zn", "inv_zn", "neg_kappa", "two_cz", "inv_two_cz", "neg_ln_two_cz", "cz_sq",
+                "two_zn", "neg_two_zn", "neg_inv_zn_sq",
+            )
+        ]
 
         with tc.tile_pool(name="setup", bufs=2) as setup:
             vector_rows = setup.tile([P, P], BF16, bufs=1)
             nc.vector.memset(vector_rows[:], 0.0)
             nc.sync.dma_start(out=vector_rows[0:O_TILES, :], in_=r.rearrange("(t p) one -> t (p one)", p=P))
             nc.sync.dma_start(out=vector_rows[O_TILES : 2 * O_TILES, :], in_=bias.rearrange("(t p) -> t p", p=P))
+            beta_rows = setup.tile([P, PASSES, 2 * PACK], F32, bufs=1)
+            for g in range(PASSES):
+                nc.sync.dma_start(
+                    out=beta_rows[:, g, 0:PACK],
+                    in_=beta[g * K_PASS : (g + 1) * K_PASS, :].rearrange("(q j) one -> q (j one)", j=PACK),
+                )
             z_all = setup.tile([P, O_TILES, D_MODEL], BF16, bufs=1)
             z_tiles = z.rearrange("(t p) d -> p t d", p=P)
-            quarter = O_TILES // 4
-            for first in (0, 2 * quarter, quarter, 3 * quarter):
-                nc.sync.dma_start(out=z_all[:, first : first + quarter, :], in_=z_tiles[:, first : first + quarter, :])
-            beta_rows = setup.tile([P, TOKENS], F32, bufs=1)
-            nc.sync.dma_start(out=beta_rows[:], in_=beta.rearrange("b one -> (b one)").partition_broadcast(P))
+
+            def load_z(first, count):
+                nc.sync.dma_start(out=z_all[:, first : first + count, :], in_=z_tiles[:, first : first + count, :])
+
             for batch in range(2):
+                load_z(batch * BATCH, BATCH)
                 xz_rows[batch] = load_token_rows(early, xz, F32, batch * BATCH * P, BATCH * P, "xz_rows")
+            for first in range(2 * BATCH, O_TILES, 4):
+                load_z(first, 4)
             x_raw = {}
             for g in range(PASSES):
                 x_raw[g] = setup.tile([P, PACK, D_MODEL], BF16, name="x_raw", tag="x_raw", bufs=PASSES)
@@ -112,56 +153,77 @@ def tile_pvfc_v_kernel(tc, x, z, r, bias, xz, beta, grad_out, out):
             nc.scalar.activation(out=exp_neg_r[:], in_=r_col, func=ACT.Exp, scale=-1.0)
             tanh_r = keep.tile([P, O_TILES], F32)
             nc.scalar.activation(out=tanh_r[:], in_=r_col, func=ACT.Tanh)
+            two_cosh_r = keep.tile([P, O_TILES], F32)
+            nc.vector.tensor_tensor(out=two_cosh_r[:], in0=exp_r[:], in1=exp_neg_r[:], op=ALU.add)
+            half_cosh_r = keep.tile([P, O_TILES], F32)
+            nc.vector.tensor_scalar_mul(out=half_cosh_r[:], in0=two_cosh_r[:], scalar1=0.25)
+            neg_bias = keep.tile([P, O_TILES], F32)
+            nc.vector.tensor_scalar_mul(out=neg_bias[:], in0=bias_col, scalar1=-1.0)
 
-            zn_sq = keep.tile([P, O_TILES], F32)
-            for i in range(O_TILES // 2):
-                t = i
-                squares = setup.tile([P, D_MODEL], F32, name="squares_v", tag="squares_v")
+            beta_all = keep.tile([P, TOKENS], F32)
+            for g in range(PASSES):
+                bank = psum.tile([P, K_PASS], F32, name="beta_bank", tag="feed")
+                for j in range(PACK):
+                    nc.tensor.transpose(
+                        bank[:, j * P : (j + 1) * P], beta_rows[:, g, j : j + 1].to_broadcast([P, P]), ident_f32[:]
+                    )
+                nc.vector.tensor_copy(out=beta_all[:, g * K_PASS : (g + 1) * K_PASS], in_=bank[:])
+
+            def square_norm_on_vector(t):
+                squares = setup.tile([P, D_MODEL], BF16, name="squares_v", tag="squares_v")
                 nc.vector.scalar_tensor_tensor(
                     out=squares[:], in0=z_all[:, t, :], scalar=1.0, in1=z_all[:, t, :],
                     op0=ALU.mult, op1=ALU.mult, accum_out=zn_sq[:, t : t + 1],
                 )
-                t = O_TILES // 2 + i
+
+            def square_norm_on_scalar(t):
                 squares = setup.tile([P, D_MODEL], BF16, name="squares_s", tag="squares_s")
                 nc.scalar.activation(out=squares[:], in_=z_all[:, t, :], func=ACT.Square, accum_out=zn_sq[:, t : t + 1])
-            zn = keep.tile([P, O_TILES], F32)
-            nc.scalar.activation(out=zn[:], in_=zn_sq[:], func=ACT.Sqrt)
 
-            beta_all = keep.tile([P, TOKENS], F32)
-            nc.vector.tensor_copy(
-                out=beta_all[:].rearrange("p (g j q) -> p g j q", g=PASSES, j=PACK),
-                in_=beta_rows[:].rearrange("p (g q j) -> p g j q", g=PASSES, j=PACK),
-            )
+            def feature_quantities(ts):
+                nc.gpsimd.tensor_tensor(out=zn[:, ts], in0=zn_sq[:, ts], in1=half_exponent[:, ts], op=ALU.pow)
+                nc.vector.scalar_tensor_tensor(
+                    out=neg_kappa[:, ts], in0=zn[:, ts], scalar=-1.0, in1=tanh_r[:, ts], op0=ALU.mult, op1=ALU.mult
+                )
+                nc.vector.reciprocal(out=inv_zn[:, ts], in_=zn[:, ts])
+                nc.vector.tensor_tensor(out=two_cz[:, ts], in0=two_cosh_r[:, ts], in1=inv_zn[:, ts], op=ALU.mult)
+                nc.vector.scalar_tensor_tensor(
+                    out=cz_sq[:, ts], in0=two_cz[:, ts], scalar=0.25, in1=two_cz[:, ts], op0=ALU.mult, op1=ALU.mult
+                )
+                nc.vector.reciprocal(out=inv_two_cz[:, ts], in_=two_cz[:, ts])
 
-            neg_kappa = keep.tile([P, O_TILES], F32)
-            nc.vector.scalar_tensor_tensor(
-                out=neg_kappa[:], in0=zn[:], scalar=-1.0, in1=tanh_r[:], op0=ALU.mult, op1=ALU.mult
-            )
-            inv_zn = keep.tile([P, O_TILES], F32)
-            nc.vector.reciprocal(out=inv_zn[:], in_=zn[:])
-            two_cosh_r = keep.tile([P, O_TILES], F32)
-            nc.vector.tensor_tensor(out=two_cosh_r[:], in0=exp_r[:], in1=exp_neg_r[:], op=ALU.add)
-            cz = keep.tile([P, O_TILES], F32)
-            nc.vector.scalar_tensor_tensor(
-                out=cz[:], in0=two_cosh_r[:], scalar=0.5, in1=inv_zn[:], op0=ALU.mult, op1=ALU.mult
-            )
-            cz_sq = keep.tile([P, O_TILES], F32)
-            nc.vector.tensor_tensor(out=cz_sq[:], in0=cz[:], in1=cz[:], op=ALU.mult)
+            def feature_logs(ts):
+                nc.scalar.activation(out=neg_ln_two_cz[:, ts], in_=inv_two_cz[:, ts], func=ACT.Ln)
+
+            def more_feature_quantities(ts):
+                nc.vector.tensor_scalar_mul(out=two_zn[:, ts], in0=zn[:, ts], scalar1=2.0)
+                nc.vector.tensor_scalar_mul(out=neg_two_zn[:, ts], in0=zn[:, ts], scalar1=-2.0)
+                nc.vector.scalar_tensor_tensor(
+                    out=neg_inv_zn_sq[:, ts], in0=inv_zn[:, ts], scalar=-1.0, in1=inv_zn[:, ts],
+                    op0=ALU.mult, op1=ALU.mult,
+                )
+
+            first_tiles, other_tiles = slice(0, 2 * BATCH), slice(2 * BATCH, O_TILES)
+            for t in range(BATCH):
+                square_norm_on_vector(t)
+            feature_quantities(slice(0, BATCH))
+            for t in range(BATCH, 2 * BATCH):
+                square_norm_on_scalar(t)
             for t in range(BATCH):
                 shifted_xz(t)
-
-            two_zn = keep.tile([P, O_TILES], F32)
-            nc.vector.tensor_scalar_mul(out=two_zn[:], in0=zn[:], scalar1=2.0)
-            neg_two_zn = keep.tile([P, O_TILES], F32)
-            nc.vector.tensor_scalar_mul(out=neg_two_zn[:], in0=zn[:], scalar1=-2.0)
-            neg_bias = keep.tile([P, O_TILES], F32)
-            nc.vector.tensor_scalar_mul(out=neg_bias[:], in0=bias_col, scalar1=-1.0)
-            half_cosh_r = keep.tile([P, O_TILES], F32)
-            nc.vector.tensor_scalar_mul(out=half_cosh_r[:], in0=two_cosh_r[:], scalar1=0.25)
-            neg_inv_zn_sq = keep.tile([P, O_TILES], F32)
-            nc.vector.scalar_tensor_tensor(
-                out=neg_inv_zn_sq[:], in0=inv_zn[:], scalar=-1.0, in1=inv_zn[:], op0=ALU.mult, op1=ALU.mult
-            )
+            feature_quantities(slice(BATCH, 2 * BATCH))
+            more_feature_quantities(first_tiles)
+            for t in range(BATCH):
+                first_log(t)
+            feature_logs(first_tiles)
+            for t in range(BATCH):
+                root(t)
+            for t in range(O_TILES - 2, O_TILES):
+                square_norm_on_scalar(t)
+            for t in range(2 * BATCH, O_TILES - 2):
+                square_norm_on_vector(t)
+            for t in range(BATCH, 2 * BATCH):
+                shifted_xz(t)
 
             x_codes = keep.tile([P, PASSES, D_MODEL], U32, align_bytes=64)
             x_scales = keep.tile([P, PASSES, D_MODEL], U8, align_bytes=64)
@@ -201,17 +263,8 @@ def tile_pvfc_v_kernel(tc, x, z, r, bias, xz, beta, grad_out, out):
             load_xz_again(first_two)
             load_z_tile(first_two)
 
-        def first_log(t):
-            asinh[t] = early.tile([P, TOKENS], F32, name="asinh", tag="asinh", bufs=3 * BATCH)
-            nc.scalar.activation(out=asinh[t][:], in_=y[t][:], func=ACT.Abs, scale=cz[:, t : t + 1])
-            nc.scalar.activation(out=log1p_sq[t][:], in_=log1p_sq[t][:], func=ACT.Ln, scale=cz_sq[:, t : t + 1], bias=one[:])
-
-        def root(t):
-            nc.scalar.activation(out=y[t][:], in_=log1p_sq[t][:], func=ACT.Exp, scale=0.5)
-            nc.gpsimd.tensor_tensor(out=asinh[t][:], in0=asinh[t][:], in1=y[t][:], op=ALU.add)
-
         def second_log(t):
-            nc.scalar.activation(out=asinh[t][:], in_=asinh[t][:], func=ACT.Ln)
+            nc.scalar.activation(out=asinh[t][:], in_=asinh[t][:], func=ACT.Ln, scale=two_cz[:, t : t + 1])
             nc.gpsimd.tensor_tensor(out=asinh[t][:], in0=asinh[t][:], in1=half_sign[t][:], op=ALU.mult)
 
         def exponentials(t):
@@ -326,13 +379,18 @@ def tile_pvfc_v_kernel(tc, x, z, r, bias, xz, beta, grad_out, out):
             if 0 <= t < O_TILES:
                 stage(t)
 
-        for k in range(-1, BATCHES + 2):
+        for k in range(BATCHES + 2):
             t = BATCH * k
             run(grad_v, t - 2)
             run(finish, t - 3)
             run(grad_xz, t - 2)
             run(second_log, t)
             run(second_log, t + 1)
+            if k == 1:
+                feature_logs(other_tiles)
+            if k == 0:
+                feature_quantities(other_tiles)
+                more_feature_quantities(other_tiles)
             run(first_log, t + 2)
             run(quantise_dxz, t - 2)
             run(first_log, t + 3)

@@ -63,6 +63,9 @@ def tile_pvfc_v_kernel(tc, x, z, r, bias, xz, beta, grad_out, out):
                 nc.tensor.transpose(bank[:, j * P : (j + 1) * P], block[:, j, :], ident_f32[:])
             return bank
 
+        def half_abs_by_gpsimd(t):
+            return t >= BATCH and t % 2 == 1
+
         def shifted_xz(t):
             batch, place = divmod(t, BATCH)
             y[t] = early.tile([P, TOKENS], F32, name="y", tag="y")
@@ -78,32 +81,33 @@ def tile_pvfc_v_kernel(tc, x, z, r, bias, xz, beta, grad_out, out):
                 out=half_sign[t][:], in0=y[t][:], scalar1=0.0, scalar2=0.5, op0=ALU.is_ge, op1=ALU.subtract
             )
             log1p_sq[t] = early.tile([P, TOKENS], F32, name="log1p_sq", tag="log1p_sq", bufs=2 * BATCH)
-            if t < BATCH:
-                nc.scalar.activation(out=log1p_sq[t][:], in_=y[t][:], func=ACT.Square)
+            if t < 2 * BATCH:
+                nc.vector.tensor_tensor(out=log1p_sq[t][:], in0=y[t][:], in1=y[t][:], op=ALU.mult)
             else:
                 nc.gpsimd.tensor_tensor(out=log1p_sq[t][:], in0=y[t][:], in1=y[t][:], op=ALU.mult)
+            if half_abs_by_gpsimd(t):
+                asinh[t] = early.tile([P, TOKENS], F32, name="asinh", tag="asinh", bufs=3 * BATCH)
+                nc.gpsimd.tensor_tensor(out=asinh[t][:], in0=y[t][:], in1=half_sign[t][:], op=ALU.mult)
             if place == BATCH - 1 and batch + 2 < BATCHES:
                 xz_rows[batch + 2] = load_token_rows(early, xz, F32, (batch + 2) * BATCH * P, BATCH * P, "xz_rows")
 
-        def half_abs_by_gpsimd(t):
-            return t >= BATCH and t % 2 == 1
-
-        def half_abs(t):
-            asinh[t] = early.tile([P, TOKENS], F32, name="asinh", tag="asinh", bufs=3 * BATCH)
-            if half_abs_by_gpsimd(t):
-                nc.gpsimd.tensor_tensor(out=asinh[t][:], in0=y[t][:], in1=half_sign[t][:], op=ALU.mult)
-            else:
-                nc.scalar.activation(out=asinh[t][:], in_=y[t][:], func=ACT.Abs, scale=0.5)
+        def pieces(t):
+            if t >= BATCH:
+                return [slice(0, TOKENS)]
+            return [slice(g * K_PASS, (g + 1) * K_PASS) for g in range(PASSES)]
 
         def first_log(t):
-            half_abs(t)
+            if not half_abs_by_gpsimd(t):
+                asinh[t] = early.tile([P, TOKENS], F32, name="asinh", tag="asinh", bufs=3 * BATCH)
+                nc.scalar.activation(out=asinh[t][:], in_=y[t][:], func=ACT.Abs, scale=0.5)
             nc.scalar.activation(out=log1p_sq[t][:], in_=log1p_sq[t][:], func=ACT.Ln, scale=cz_sq[:, t : t + 1], bias=one[:])
 
         def root(t):
-            nc.scalar.activation(
-                out=y[t][:], in_=log1p_sq[t][:], func=ACT.Exp, scale=0.5, bias=neg_ln_two_cz[:, t : t + 1]
-            )
-            nc.gpsimd.tensor_tensor(out=asinh[t][:], in0=asinh[t][:], in1=y[t][:], op=ALU.add)
+            for cols in pieces(t):
+                nc.scalar.activation(
+                    out=y[t][:, cols], in_=log1p_sq[t][:, cols], func=ACT.Exp, scale=0.5, bias=neg_ln_two_cz[:, t : t + 1]
+                )
+                nc.gpsimd.tensor_tensor(out=asinh[t][:, cols], in0=asinh[t][:, cols], in1=y[t][:, cols], op=ALU.add)
 
         zn_sq, zn, inv_zn, neg_kappa, two_cz, inv_two_cz, neg_ln_two_cz, cz_sq, two_zn, neg_two_zn, neg_inv_zn_sq = [
             keep.tile([P, O_TILES], F32, name=name, tag=name)
@@ -180,8 +184,10 @@ def tile_pvfc_v_kernel(tc, x, z, r, bias, xz, beta, grad_out, out):
                 squares = setup.tile([P, D_MODEL], BF16, name="squares_s", tag="squares_s")
                 nc.scalar.activation(out=squares[:], in_=z_all[:, t, :], func=ACT.Square, accum_out=zn_sq[:, t : t + 1])
 
-            def feature_quantities(ts):
+            def norms(ts):
                 nc.gpsimd.tensor_tensor(out=zn[:, ts], in0=zn_sq[:, ts], in1=half_exponent[:, ts], op=ALU.pow)
+
+            def feature_quantities(ts):
                 nc.vector.scalar_tensor_tensor(
                     out=neg_kappa[:, ts], in0=zn[:, ts], scalar=-1.0, in1=tanh_r[:, ts], op0=ALU.mult, op1=ALU.mult
                 )
@@ -203,14 +209,16 @@ def tile_pvfc_v_kernel(tc, x, z, r, bias, xz, beta, grad_out, out):
                     op0=ALU.mult, op1=ALU.mult,
                 )
 
-            first_tiles, other_tiles = slice(0, 2 * BATCH), slice(2 * BATCH, O_TILES)
+            first_tiles, next_tiles, other_tiles = slice(0, 2 * BATCH), slice(2 * BATCH, 4 * BATCH), slice(4 * BATCH, O_TILES)
             for t in range(BATCH):
                 square_norm_on_vector(t)
+            norms(slice(0, BATCH))
             feature_quantities(slice(0, BATCH))
             for t in range(BATCH, 2 * BATCH):
                 square_norm_on_scalar(t)
             for t in range(BATCH):
                 shifted_xz(t)
+            norms(slice(BATCH, 2 * BATCH))
             feature_quantities(slice(BATCH, 2 * BATCH))
             more_feature_quantities(first_tiles)
             for t in range(BATCH):
@@ -220,10 +228,12 @@ def tile_pvfc_v_kernel(tc, x, z, r, bias, xz, beta, grad_out, out):
                 root(t)
             for t in range(O_TILES - 2, O_TILES):
                 square_norm_on_scalar(t)
-            for t in range(2 * BATCH, O_TILES - 2):
+            for t in range(2 * BATCH, 4 * BATCH + 2):
                 square_norm_on_vector(t)
             for t in range(BATCH, 2 * BATCH):
                 shifted_xz(t)
+            for t in range(4 * BATCH + 2, O_TILES - 2):
+                square_norm_on_vector(t)
 
             x_codes = keep.tile([P, PASSES, D_MODEL], U32, align_bytes=64)
             x_scales = keep.tile([P, PASSES, D_MODEL], U8, align_bytes=64)
@@ -264,8 +274,9 @@ def tile_pvfc_v_kernel(tc, x, z, r, bias, xz, beta, grad_out, out):
             load_z_tile(first_two)
 
         def second_log(t):
-            nc.scalar.activation(out=asinh[t][:], in_=asinh[t][:], func=ACT.Ln, scale=two_cz[:, t : t + 1])
-            nc.gpsimd.tensor_tensor(out=asinh[t][:], in0=asinh[t][:], in1=half_sign[t][:], op=ALU.mult)
+            for cols in pieces(t):
+                nc.scalar.activation(out=asinh[t][:, cols], in_=asinh[t][:, cols], func=ACT.Ln, scale=two_cz[:, t : t + 1])
+                nc.gpsimd.tensor_tensor(out=asinh[t][:, cols], in0=asinh[t][:, cols], in1=half_sign[t][:, cols], op=ALU.mult)
 
         def exponentials(t):
             inv_root[t] = late.tile([P, TOKENS], F32, name="inv_root", tag="inv_root")
@@ -386,11 +397,10 @@ def tile_pvfc_v_kernel(tc, x, z, r, bias, xz, beta, grad_out, out):
             run(grad_xz, t - 2)
             run(second_log, t)
             run(second_log, t + 1)
-            if k == 1:
-                feature_logs(other_tiles)
             if k == 0:
-                feature_quantities(other_tiles)
-                more_feature_quantities(other_tiles)
+                norms(next_tiles)
+            if 1 <= k <= 2:
+                feature_logs(next_tiles if k == 1 else other_tiles)
             run(first_log, t + 2)
             run(quantise_dxz, t - 2)
             run(first_log, t + 3)
@@ -402,5 +412,10 @@ def tile_pvfc_v_kernel(tc, x, z, r, bias, xz, beta, grad_out, out):
             run(exponentials, t)
             run(quantise_dxz, t - 1)
             run(exponentials, t + 1)
+            if k < 2:
+                feature_quantities(next_tiles if k == 0 else other_tiles)
+                more_feature_quantities(next_tiles if k == 0 else other_tiles)
             run(shifted_xz, t + 4)
             run(shifted_xz, t + 5)
+            if k == 0:
+                norms(other_tiles)

@@ -24,7 +24,6 @@ BATCH = 2
 BATCHES = O_TILES // BATCH
 N_TILE = 512
 D_HALVES = D_MODEL // N_TILE
-BANKS_EMPTIED_BY_SCALAR = 1
 
 
 def tile_pvfc_v_kernel(tc, x, z, r, bias, xz, beta, grad_out, out):
@@ -52,8 +51,24 @@ def tile_pvfc_v_kernel(tc, x, z, r, bias, xz, beta, grad_out, out):
         make_identity(nc, ident_bf16[:])
         one = keep.tile([P, 1], F32)
         nc.vector.memset(one[:], 1.0)
-        half_exponent = keep.tile([P, O_TILES], F32)
-        nc.vector.memset(half_exponent[:], 0.5)
+
+        def per_feature(name):
+            return keep.tile([P, O_TILES], F32, name=name, tag=name)
+
+        def constant(name, value):
+            tile = per_feature(name)
+            nc.vector.memset(tile[:], value)
+            return tile
+
+        half, minus_half, minus_one, minus_two = [
+            constant(name, value)
+            for name, value in (("half", 0.5), ("minus_half", -0.5), ("minus_one", -1.0), ("minus_two", -2.0))
+        ]
+        zn_sq, zn, inv_zn, neg_inv_zn, neg_inv_zn_sq, two_zn, neg_two_zn = [
+            per_feature(name)
+            for name in ("zn_sq", "zn", "inv_zn", "neg_inv_zn", "neg_inv_zn_sq", "two_zn", "neg_two_zn")
+        ]
+        neg_kappa, cz, cz_sq = [per_feature(name) for name in ("neg_kappa", "cz", "cz_sq")]
 
         xz_rows, y, log1p_sq, asinh, half_sign = {}, {}, {}, {}, {}
 
@@ -63,8 +78,16 @@ def tile_pvfc_v_kernel(tc, x, z, r, bias, xz, beta, grad_out, out):
                 nc.tensor.transpose(bank[:, j * P : (j + 1) * P], block[:, j, :], ident_f32[:])
             return bank
 
-        def half_abs_by_gpsimd(t):
-            return t >= BATCH and t % 2 == 1
+        def fills_the_pipeline(t):
+            return t < BATCH
+
+        def pieces(t):
+            if not fills_the_pipeline(t):
+                return [slice(0, TOKENS)]
+            return [slice(g * K_PASS, (g + 1) * K_PASS) for g in range(PASSES)]
+
+        def for_sbuf_pairs(t):
+            return nc.vector if fills_the_pipeline(t) else nc.gpsimd
 
         def shifted_xz(t):
             batch, place = divmod(t, BATCH)
@@ -76,46 +99,39 @@ def tile_pvfc_v_kernel(tc, x, z, r, bias, xz, beta, grad_out, out):
                     out=y[t][:, tokens], in0=beta_all[:, tokens], scalar=neg_kappa[:, t : t + 1],
                     in1=bank[:], op0=ALU.mult, op1=ALU.add,
                 )
+            if place == BATCH - 1 and batch + 2 < BATCHES:
+                xz_rows[batch + 2] = load_token_rows(early, xz, F32, (batch + 2) * BATCH * P, BATCH * P, "xz_rows")
+
+        def sign(t):
             half_sign[t] = early.tile([P, TOKENS], BF16, name="half_sign", tag="half_sign", bufs=2 * BATCH)
             nc.vector.tensor_scalar(
                 out=half_sign[t][:], in0=y[t][:], scalar1=0.0, scalar2=0.5, op0=ALU.is_ge, op1=ALU.subtract
             )
-            log1p_sq[t] = early.tile([P, TOKENS], F32, name="log1p_sq", tag="log1p_sq", bufs=2 * BATCH)
-            if t < 2 * BATCH:
-                nc.vector.tensor_tensor(out=log1p_sq[t][:], in0=y[t][:], in1=y[t][:], op=ALU.mult)
-            else:
-                nc.gpsimd.tensor_tensor(out=log1p_sq[t][:], in0=y[t][:], in1=y[t][:], op=ALU.mult)
-            if half_abs_by_gpsimd(t):
-                asinh[t] = early.tile([P, TOKENS], F32, name="asinh", tag="asinh", bufs=3 * BATCH)
-                nc.gpsimd.tensor_tensor(out=asinh[t][:], in0=y[t][:], in1=half_sign[t][:], op=ALU.mult)
-            if place == BATCH - 1 and batch + 2 < BATCHES:
-                xz_rows[batch + 2] = load_token_rows(early, xz, F32, (batch + 2) * BATCH * P, BATCH * P, "xz_rows")
 
-        def pieces(t):
-            if t >= BATCH:
-                return [slice(0, TOKENS)]
-            return [slice(g * K_PASS, (g + 1) * K_PASS) for g in range(PASSES)]
+        def square(t):
+            log1p_sq[t] = early.tile([P, TOKENS], F32, name="log1p_sq", tag="log1p_sq", bufs=2 * BATCH)
+            engine = nc.vector if t < 2 * BATCH else nc.gpsimd
+            engine.tensor_tensor(out=log1p_sq[t][:], in0=y[t][:], in1=y[t][:], op=ALU.mult)
 
         def first_log(t):
-            if not half_abs_by_gpsimd(t):
-                asinh[t] = early.tile([P, TOKENS], F32, name="asinh", tag="asinh", bufs=3 * BATCH)
-                nc.scalar.activation(out=asinh[t][:], in_=y[t][:], func=ACT.Abs, scale=0.5)
+            asinh[t] = early.tile([P, TOKENS], F32, name="asinh", tag="asinh", bufs=3 * BATCH)
+            nc.scalar.activation(out=asinh[t][:], in_=y[t][:], func=ACT.Abs, scale=cz[:, t : t + 1])
             nc.scalar.activation(out=log1p_sq[t][:], in_=log1p_sq[t][:], func=ACT.Ln, scale=cz_sq[:, t : t + 1], bias=one[:])
 
         def root(t):
+            root_tile = early.tile([P, TOKENS], F32, name="root", tag="root")
             for cols in pieces(t):
-                nc.scalar.activation(
-                    out=y[t][:, cols], in_=log1p_sq[t][:, cols], func=ACT.Exp, scale=0.5, bias=neg_ln_two_cz[:, t : t + 1]
+                nc.scalar.activation(out=root_tile[:, cols], in_=log1p_sq[t][:, cols], func=ACT.Exp, scale=0.5)
+                for_sbuf_pairs(t).tensor_tensor(
+                    out=asinh[t][:, cols], in0=asinh[t][:, cols], in1=root_tile[:, cols], op=ALU.add
                 )
-                nc.gpsimd.tensor_tensor(out=asinh[t][:, cols], in0=asinh[t][:, cols], in1=y[t][:, cols], op=ALU.add)
 
-        zn_sq, zn, inv_zn, neg_kappa, two_cz, inv_two_cz, neg_ln_two_cz, cz_sq, two_zn, neg_two_zn, neg_inv_zn_sq = [
-            keep.tile([P, O_TILES], F32, name=name, tag=name)
-            for name in (
-                "zn_sq", "zn", "inv_zn", "neg_kappa", "two_cz", "inv_two_cz", "neg_ln_two_cz", "cz_sq",
-                "two_zn", "neg_two_zn", "neg_inv_zn_sq",
-            )
-        ]
+        def second_log(t):
+            for cols in pieces(t):
+                nc.scalar.activation(out=asinh[t][:, cols], in_=asinh[t][:, cols], func=ACT.Ln)
+                for_sbuf_pairs(t).tensor_tensor(
+                    out=asinh[t][:, cols], in0=asinh[t][:, cols], in1=half_sign[t][:, cols], op=ALU.mult
+                )
 
         with tc.tile_pool(name="setup", bufs=2) as setup:
             vector_rows = setup.tile([P, P], BF16, bufs=1)
@@ -151,17 +167,19 @@ def tile_pvfc_v_kernel(tc, x, z, r, bias, xz, beta, grad_out, out):
             r_col = r_and_bias[:, 0:O_TILES]
             bias_col = r_and_bias[:, O_TILES : 2 * O_TILES]
 
-            exp_r = keep.tile([P, O_TILES], F32)
+            exp_r = per_feature("exp_r")
             nc.scalar.activation(out=exp_r[:], in_=r_col, func=ACT.Exp)
-            exp_neg_r = keep.tile([P, O_TILES], F32)
+            exp_neg_r = per_feature("exp_neg_r")
             nc.scalar.activation(out=exp_neg_r[:], in_=r_col, func=ACT.Exp, scale=-1.0)
-            tanh_r = keep.tile([P, O_TILES], F32)
-            nc.scalar.activation(out=tanh_r[:], in_=r_col, func=ACT.Tanh)
-            two_cosh_r = keep.tile([P, O_TILES], F32)
+            neg_tanh_r = per_feature("neg_tanh_r")
+            nc.scalar.activation(out=neg_tanh_r[:], in_=r_col, func=ACT.Tanh, scale=-1.0)
+            two_cosh_r = per_feature("two_cosh_r")
             nc.vector.tensor_tensor(out=two_cosh_r[:], in0=exp_r[:], in1=exp_neg_r[:], op=ALU.add)
-            half_cosh_r = keep.tile([P, O_TILES], F32)
+            cosh_r = per_feature("cosh_r")
+            nc.vector.tensor_scalar_mul(out=cosh_r[:], in0=two_cosh_r[:], scalar1=0.5)
+            half_cosh_r = per_feature("half_cosh_r")
             nc.vector.tensor_scalar_mul(out=half_cosh_r[:], in0=two_cosh_r[:], scalar1=0.25)
-            neg_bias = keep.tile([P, O_TILES], F32)
+            neg_bias = per_feature("neg_bias")
             nc.vector.tensor_scalar_mul(out=neg_bias[:], in0=bias_col, scalar1=-1.0)
 
             beta_all = keep.tile([P, TOKENS], F32)
@@ -184,56 +202,49 @@ def tile_pvfc_v_kernel(tc, x, z, r, bias, xz, beta, grad_out, out):
                 squares = setup.tile([P, D_MODEL], BF16, name="squares_s", tag="squares_s")
                 nc.scalar.activation(out=squares[:], in_=z_all[:, t, :], func=ACT.Square, accum_out=zn_sq[:, t : t + 1])
 
-            def norms(ts):
-                nc.gpsimd.tensor_tensor(out=zn[:, ts], in0=zn_sq[:, ts], in1=half_exponent[:, ts], op=ALU.pow)
+            def feature_quantities(ts, engine):
+                nc.gpsimd.tensor_tensor(out=zn[:, ts], in0=zn_sq[:, ts], in1=half[:, ts], op=ALU.pow)
+                nc.gpsimd.tensor_tensor(out=inv_zn[:, ts], in0=zn_sq[:, ts], in1=minus_half[:, ts], op=ALU.pow)
+                for result, a, b, op in (
+                    (neg_kappa, zn, neg_tanh_r, ALU.mult),
+                    (cz, cosh_r, inv_zn, ALU.mult),
+                    (cz_sq, cz, cz, ALU.mult),
+                    (two_zn, zn, zn, ALU.add),
+                    (neg_two_zn, zn, minus_two, ALU.mult),
+                    (neg_inv_zn, inv_zn, minus_one, ALU.mult),
+                    (neg_inv_zn_sq, neg_inv_zn, inv_zn, ALU.mult),
+                ):
+                    engine.tensor_tensor(out=result[:, ts], in0=a[:, ts], in1=b[:, ts], op=op)
 
-            def feature_quantities(ts):
-                nc.vector.scalar_tensor_tensor(
-                    out=neg_kappa[:, ts], in0=zn[:, ts], scalar=-1.0, in1=tanh_r[:, ts], op0=ALU.mult, op1=ALU.mult
-                )
-                nc.vector.reciprocal(out=inv_zn[:, ts], in_=zn[:, ts])
-                nc.vector.tensor_tensor(out=two_cz[:, ts], in0=two_cosh_r[:, ts], in1=inv_zn[:, ts], op=ALU.mult)
-                nc.vector.scalar_tensor_tensor(
-                    out=cz_sq[:, ts], in0=two_cz[:, ts], scalar=0.25, in1=two_cz[:, ts], op0=ALU.mult, op1=ALU.mult
-                )
-                nc.vector.reciprocal(out=inv_two_cz[:, ts], in_=two_cz[:, ts])
-
-            def feature_logs(ts):
-                nc.scalar.activation(out=neg_ln_two_cz[:, ts], in_=inv_two_cz[:, ts], func=ACT.Ln)
-
-            def more_feature_quantities(ts):
-                nc.vector.tensor_scalar_mul(out=two_zn[:, ts], in0=zn[:, ts], scalar1=2.0)
-                nc.vector.tensor_scalar_mul(out=neg_two_zn[:, ts], in0=zn[:, ts], scalar1=-2.0)
-                nc.vector.scalar_tensor_tensor(
-                    out=neg_inv_zn_sq[:, ts], in0=inv_zn[:, ts], scalar=-1.0, in1=inv_zn[:, ts],
-                    op0=ALU.mult, op1=ALU.mult,
-                )
-
-            first_tiles, next_tiles, other_tiles = slice(0, 2 * BATCH), slice(2 * BATCH, 4 * BATCH), slice(4 * BATCH, O_TILES)
+            next_tiles, other_tiles = slice(2 * BATCH, 4 * BATCH), slice(4 * BATCH, O_TILES)
             for t in range(BATCH):
                 square_norm_on_vector(t)
-            norms(slice(0, BATCH))
-            feature_quantities(slice(0, BATCH))
+            feature_quantities(slice(0, BATCH), nc.vector)
             for t in range(BATCH, 2 * BATCH):
                 square_norm_on_scalar(t)
             for t in range(BATCH):
                 shifted_xz(t)
-            norms(slice(BATCH, 2 * BATCH))
-            feature_quantities(slice(BATCH, 2 * BATCH))
-            more_feature_quantities(first_tiles)
-            for t in range(BATCH):
+                square(t)
                 first_log(t)
-            feature_logs(first_tiles)
+            feature_quantities(slice(BATCH, 2 * BATCH), nc.vector)
+            for t in range(BATCH):
+                sign(t)
+            for t in range(2 * BATCH, 4 * BATCH):
+                square_norm_on_vector(t)
             for t in range(BATCH):
                 root(t)
-            for t in range(O_TILES - 2, O_TILES):
-                square_norm_on_scalar(t)
-            for t in range(2 * BATCH, 4 * BATCH + 2):
-                square_norm_on_vector(t)
+            feature_quantities(next_tiles, nc.gpsimd)
+            shifted_xz(BATCH)
+            square(BATCH)
+            second_log(0)
+            shifted_xz(BATCH + 1)
+            square(BATCH + 1)
+            second_log(1)
             for t in range(BATCH, 2 * BATCH):
-                shifted_xz(t)
-            for t in range(4 * BATCH + 2, O_TILES - 2):
-                square_norm_on_vector(t)
+                sign(t)
+                first_log(t)
+            for t in range(4 * BATCH, O_TILES):
+                square_norm_on_scalar(t)
 
             x_codes = keep.tile([P, PASSES, D_MODEL], U32, align_bytes=64)
             x_scales = keep.tile([P, PASSES, D_MODEL], U8, align_bytes=64)
@@ -241,7 +252,10 @@ def tile_pvfc_v_kernel(tc, x, z, r, bias, xz, beta, grad_out, out):
             for g in range(PASSES + 1):
                 if g < PASSES:
                     x_grouped[g] = setup.tile([P, D_MODEL, PACK], BF16, name="x_grouped", tag="x_grouped", align_bytes=64)
-                    nc.vector.tensor_copy(out=x_grouped[g][:], in_=x_raw[g][:].rearrange("p j d -> p d j"))
+                    nc.vector.tensor_copy(
+                        out=x_grouped[g][:].rearrange("p (c i) j -> p c j i", i=4),
+                        in_=x_raw[g][:].rearrange("p j (c i) -> p c j i", i=4),
+                    )
                 if g > 0:
                     nc.vector.quantize_mx(
                         out=x_codes[:, g - 1, :].bitcast(E4M3_X4),
@@ -250,7 +264,7 @@ def tile_pvfc_v_kernel(tc, x, z, r, bias, xz, beta, grad_out, out):
                     )
 
         late = stack.enter_context(tc.tile_pool(name="late", bufs=2, reuse_waits="tile"))
-        inv_root, exp_v, exp_neg_v, dxz, back_banks, dxz_codes, dxz_scales = {}, {}, {}, {}, {}, {}, {}
+        inv_root, exp_v, exp_neg_v, dxz, back_banks, grouped, dxz_codes, dxz_scales = {}, {}, {}, {}, {}, {}, {}, {}
         g_rows, xz_again, z_tile, dv2_rows = {}, {}, {}, {}
         t_parts = keep.tile([P, O_TILES, 2 * PASSES], F32)
         t_over_zn = keep.tile([P, O_TILES], F32)
@@ -265,22 +279,17 @@ def tile_pvfc_v_kernel(tc, x, z, r, bias, xz, beta, grad_out, out):
 
         def load_z_tile(t):
             if t < O_TILES:
-                z_tile[t] = late.tile([P, D_MODEL], BF16, name="z_tile", tag="z_tile")
+                z_tile[t] = late.tile([P, D_MODEL], BF16, name="z_tile", tag="z_tile", bufs=Z_BUFS)
                 nc.sync.dma_start(out=z_tile[t][:], in_=z[t * P : (t + 1) * P, :])
 
+        Z_BUFS = BATCH + 1
         for first_two in range(2):
             load_g_rows(first_two)
             load_xz_again(first_two)
-            load_z_tile(first_two)
-
-        def second_log(t):
-            for cols in pieces(t):
-                nc.scalar.activation(out=asinh[t][:, cols], in_=asinh[t][:, cols], func=ACT.Ln, scale=two_cz[:, t : t + 1])
-                nc.gpsimd.tensor_tensor(out=asinh[t][:, cols], in0=asinh[t][:, cols], in1=half_sign[t][:, cols], op=ALU.mult)
+        for t in range(Z_BUFS):
+            load_z_tile(t)
 
         def exponentials(t):
-            inv_root[t] = late.tile([P, TOKENS], F32, name="inv_root", tag="inv_root")
-            nc.scalar.activation(out=inv_root[t][:], in_=log1p_sq[t][:], func=ACT.Exp, scale=-0.5)
             exp_v[t] = late.tile([P, TOKENS], F32, name="exp_v", tag="exp_v")
             nc.scalar.activation(
                 out=exp_v[t][:], in_=asinh[t][:], func=ACT.Exp, scale=two_zn[:, t : t + 1], bias=bias_col[:, t : t + 1]
@@ -290,10 +299,12 @@ def tile_pvfc_v_kernel(tc, x, z, r, bias, xz, beta, grad_out, out):
                 out=exp_neg_v[t][:], in_=asinh[t][:], func=ACT.Exp,
                 scale=neg_two_zn[:, t : t + 1], bias=neg_bias[:, t : t + 1],
             )
+            inv_root[t] = late.tile([P, TOKENS], F32, name="inv_root", tag="inv_root")
+            nc.scalar.activation(out=inv_root[t][:], in_=log1p_sq[t][:], func=ACT.Exp, scale=-0.5)
 
         def grad_v(t):
             batch, place = divmod(t, BATCH)
-            dv2_rows[t] = late.tile([P, PASSES, PACK, P], F32, name="dv2_rows", tag="dv2_rows")
+            dv2_rows[t] = late.tile([P, PASSES, PACK, P], F32, name="dv2_rows", tag="dv2_rows", bufs=1)
             for g in range(PASSES):
                 bank = psum.tile([P, K_PASS], F32, name="cosh_bank", tag="feed")
                 for j in range(PACK):
@@ -314,7 +325,7 @@ def tile_pvfc_v_kernel(tc, x, z, r, bias, xz, beta, grad_out, out):
                 load_g_rows(batch + 2)
 
         def grad_xz(t):
-            dxz[t] = late.tile([P, TOKENS], F32, name="dxz", tag="dxz")
+            dxz[t] = late.tile([P, TOKENS], F32, name="dxz", tag="dxz", bufs=1)
             for g in range(PASSES):
                 tokens = slice(g * K_PASS, (g + 1) * K_PASS)
                 bank = psum.tile([P, K_PASS], F32, name="dv2_bank", tag="feed")
@@ -324,15 +335,17 @@ def tile_pvfc_v_kernel(tc, x, z, r, bias, xz, beta, grad_out, out):
                     out=dxz[t][:, tokens], in0=bank[:], scalar=half_cosh_r[:, t : t + 1], in1=inv_root[t][:, tokens],
                     op0=ALU.mult, op1=ALU.mult,
                 )
+                products = late.tile([P, K_PASS], BF16, name="products", tag="products")
                 nc.vector.scalar_tensor_tensor(
-                    out=exp_v[t][:, tokens], in0=bank[:], scalar=inv_zn[:, t : t + 1], in1=asinh[t][:, tokens],
+                    out=products[:], in0=bank[:], scalar=inv_zn[:, t : t + 1], in1=asinh[t][:, tokens],
                     op0=ALU.mult, op1=ALU.mult, accum_out=t_parts[:, t, g : g + 1],
                 )
             for g in range(PASSES):
                 tokens = slice(g * K_PASS, (g + 1) * K_PASS)
                 bank = xz_pass_to_o_layout(xz_again[t][:, g, :, :])
+                products = late.tile([P, K_PASS], BF16, name="products", tag="products")
                 nc.vector.scalar_tensor_tensor(
-                    out=exp_neg_v[t][:, tokens], in0=dxz[t][:, tokens], scalar=neg_inv_zn_sq[:, t : t + 1], in1=bank[:],
+                    out=products[:], in0=dxz[t][:, tokens], scalar=neg_inv_zn_sq[:, t : t + 1], in1=bank[:],
                     op0=ALU.mult, op1=ALU.mult, accum_out=t_parts[:, t, PASSES + g : PASSES + g + 1],
                 )
             load_xz_again(t + 2)
@@ -344,30 +357,37 @@ def tile_pvfc_v_kernel(tc, x, z, r, bias, xz, beta, grad_out, out):
                     nc.tensor.transpose(bank[:, j * P : (j + 1) * P], dxz[t][:, first : first + P], ident_f32[:])
                 back_banks[t].append(bank)
 
+        def banks_emptied_by_scalar(t):
+            return 0 if t < O_TILES - BATCH else PASSES
+
+        def group_dxz(t, g, copy):
+            copy(out=grouped[t][:, g, :, :], in_=back_banks[t][g][:].rearrange("p (j o) -> p o j", j=PACK))
+
+        def group_on_vector(t):
+            grouped[t] = late.tile([P, PASSES, P, PACK], BF16, name="dxz_grouped", tag="dxz_grouped", align_bytes=64)
+            for g in range(banks_emptied_by_scalar(t), PASSES):
+                group_dxz(t, g, nc.vector.tensor_copy)
+            nc.vector.tensor_reduce(
+                out=t_over_zn[:, t : t + 1], in_=t_parts[:, t, :], axis=mybir.AxisListType.X, op=ALU.add
+            )
+
+        def group_on_scalar(t):
+            for g in range(banks_emptied_by_scalar(t)):
+                group_dxz(t, g, nc.scalar.copy)
+
         def quantise_dxz(t):
-            grouped = late.tile([P, PASSES, P, PACK], BF16, name="dxz_grouped", tag="dxz_grouped", align_bytes=64)
-            for g in range(PASSES):
-                by_feature = back_banks[t][g][:].rearrange("p (j o) -> p o j", j=PACK)
-                if g < BANKS_EMPTIED_BY_SCALAR:
-                    nc.scalar.copy(out=grouped[:, g, :, :], in_=by_feature)
-                else:
-                    nc.vector.tensor_copy(out=grouped[:, g, :, :], in_=by_feature)
             dxz_codes[t] = late.tile([P, PASSES, P], U32, name="dxz_codes", tag="dxz_codes", align_bytes=64)
             dxz_scales[t] = late.tile([P, PASSES, P], U8, name="dxz_scales", tag="dxz_scales", align_bytes=64)
             for g in range(PASSES):
                 nc.vector.quantize_mx(
                     out=dxz_codes[t][:, g, :].bitcast(E5M2_X4),
                     scales=dxz_scales[t][:, g, :],
-                    in_=grouped[:, g, :, :].rearrange("p o j -> p (o j)"),
+                    in_=grouped[t][:, g, :, :].rearrange("p o j -> p (o j)"),
                 )
 
         def finish(t):
-            nc.vector.tensor_reduce(
-                out=t_over_zn[:, t : t + 1], in_=t_parts[:, t, :], axis=mybir.AxisListType.X, op=ALU.add
-            )
-            result = late.tile([P, D_MODEL], F32, name="result", tag="result")
-            for half in range(D_HALVES):
-                cols = slice(half * N_TILE, (half + 1) * N_TILE)
+            for n in range(D_HALVES):
+                cols = slice(n * N_TILE, (n + 1) * N_TILE)
                 product = psum.tile([P, N_TILE], F32, name="product", tag="back")
                 for g in range(PASSES):
                     nc.tensor.matmul_mx(
@@ -379,12 +399,13 @@ def tile_pvfc_v_kernel(tc, x, z, r, bias, xz, beta, grad_out, out):
                         start=(g == 0),
                         stop=(g == PASSES - 1),
                     )
+                result = late.tile([P, N_TILE], F32, name="result", tag="result", bufs=3)
                 nc.vector.scalar_tensor_tensor(
-                    out=result[:, cols], in0=z_tile[t][:, cols], scalar=t_over_zn[:, t : t + 1], in1=product[:],
+                    out=result[:], in0=z_tile[t][:, cols], scalar=t_over_zn[:, t : t + 1], in1=product[:],
                     op0=ALU.mult, op1=ALU.add,
                 )
-                nc.sync.dma_start(out=out[t * P : (t + 1) * P, cols], in_=result[:, cols])
-            load_z_tile(t + 2)
+                nc.sync.dma_start(out=out[t * P : (t + 1) * P, cols], in_=result[:])
+            load_z_tile(t + Z_BUFS)
 
         def run(stage, t):
             if 0 <= t < O_TILES:
@@ -393,29 +414,32 @@ def tile_pvfc_v_kernel(tc, x, z, r, bias, xz, beta, grad_out, out):
         for k in range(BATCHES + 2):
             t = BATCH * k
             run(grad_v, t - 2)
-            run(finish, t - 3)
+            run(finish, t - 4)
             run(grad_xz, t - 2)
-            run(second_log, t)
-            run(second_log, t + 1)
-            if k == 0:
-                norms(next_tiles)
-            if 1 <= k <= 2:
-                feature_logs(next_tiles if k == 1 else other_tiles)
-            run(first_log, t + 2)
-            run(quantise_dxz, t - 2)
-            run(first_log, t + 3)
-            run(grad_v, t - 1)
-            run(finish, t - 2)
-            run(grad_xz, t - 1)
-            run(root, t + 2)
-            run(root, t + 3)
-            run(exponentials, t)
-            run(quantise_dxz, t - 1)
-            run(exponentials, t + 1)
-            if k < 2:
-                feature_quantities(next_tiles if k == 0 else other_tiles)
-                more_feature_quantities(next_tiles if k == 0 else other_tiles)
+            run(group_on_vector, t - 2)
+            if k > 0:
+                run(second_log, t)
+                run(second_log, t + 1)
+            if k == 1:
+                feature_quantities(other_tiles, nc.gpsimd)
+            if k > 0:
+                run(first_log, t + 2)
+                run(first_log, t + 3)
+            run(group_on_scalar, t - 2)
             run(shifted_xz, t + 4)
             run(shifted_xz, t + 5)
-            if k == 0:
-                norms(other_tiles)
+            run(grad_v, t - 1)
+            run(quantise_dxz, t - 3)
+            run(quantise_dxz, t - 2)
+            run(sign, t + 4)
+            run(sign, t + 5)
+            run(exponentials, t)
+            run(root, t + 2)
+            run(root, t + 3)
+            run(square, t + 4)
+            run(finish, t - 3)
+            run(grad_xz, t - 1)
+            run(group_on_vector, t - 1)
+            run(exponentials, t + 1)
+            run(group_on_scalar, t - 1)
+            run(square, t + 5)

@@ -24,6 +24,9 @@ BATCH = 2
 BATCHES = O_TILES // BATCH
 N_TILE = 512
 D_HALVES = D_MODEL // N_TILE
+XZ_BUFS = 3
+Z_BUFS = BATCH + 1
+LATE_ROWS = 6
 
 
 def tile_pvfc_v_kernel(tc, x, z, r, bias, xz, beta, grad_out, out):
@@ -33,8 +36,8 @@ def tile_pvfc_v_kernel(tc, x, z, r, bias, xz, beta, grad_out, out):
         rows = matrix[g * K_PASS : (g + 1) * K_PASS, first_col : first_col + width]
         return rows.rearrange("(q j) c -> q j c", j=PACK)
 
-    def load_token_rows(pool, matrix, dtype, first_col, width, name):
-        rows = pool.tile([P, PASSES, PACK, width], dtype, name=name, tag=name)
+    def load_token_rows(pool, matrix, dtype, first_col, width, name, bufs=2):
+        rows = pool.tile([P, PASSES, PACK, width], dtype, name=name, tag=name, bufs=bufs)
         for g in range(PASSES):
             nc.sync.dma_start(out=rows[:, g, :, :], in_=pass_rows(matrix, g, first_col, width))
         return rows
@@ -43,7 +46,7 @@ def tile_pvfc_v_kernel(tc, x, z, r, bias, xz, beta, grad_out, out):
         stack.enter_context(tc.manual_schedule())
         keep = stack.enter_context(tc.tile_pool(name="keep", bufs=1))
         early = stack.enter_context(tc.tile_pool(name="early", bufs=2))
-        psum = stack.enter_context(tc.psum_pool(name="psum", bufs=4))
+        psum = stack.enter_context(tc.psum_pool(name="psum", bufs=5))
 
         ident_f32 = keep.tile([P, P], F32)
         make_identity(nc, ident_f32[:])
@@ -68,7 +71,12 @@ def tile_pvfc_v_kernel(tc, x, z, r, bias, xz, beta, grad_out, out):
             per_feature(name)
             for name in ("zn_sq", "zn", "inv_zn", "neg_inv_zn", "neg_inv_zn_sq", "two_zn", "neg_two_zn")
         ]
-        neg_kappa, cz, cz_sq = [per_feature(name) for name in ("neg_kappa", "cz", "cz_sq")]
+        ln_zn, ln_half_cz, bias_v, bias_neg_v, t_sum = [
+            per_feature(name) for name in ("ln_zn", "ln_half_cz", "bias_v", "bias_neg_v", "t_sum")
+        ]
+        neg_kappa, cz, cz_sq, inv_cz, neg_ln_cz = [
+            per_feature(name) for name in ("neg_kappa", "cz", "cz_sq", "inv_cz", "neg_ln_cz")
+        ]
 
         xz_rows, y, log1p_sq, asinh, half_sign = {}, {}, {}, {}, {}
 
@@ -82,7 +90,7 @@ def tile_pvfc_v_kernel(tc, x, z, r, bias, xz, beta, grad_out, out):
             return t < BATCH
 
         def pieces(t):
-            if not fills_the_pipeline(t):
+            if BATCH <= t < O_TILES - BATCH:
                 return [slice(0, TOKENS)]
             return [slice(g * K_PASS, (g + 1) * K_PASS) for g in range(PASSES)]
 
@@ -90,23 +98,32 @@ def tile_pvfc_v_kernel(tc, x, z, r, bias, xz, beta, grad_out, out):
             return nc.vector if fills_the_pipeline(t) else nc.gpsimd
 
         def shifted_xz(t):
-            batch, place = divmod(t, BATCH)
-            y[t] = early.tile([P, TOKENS], F32, name="y", tag="y")
+            y[t] = early.tile([P, TOKENS], F32, name="y", tag="y", bufs=XZ_BUFS)
             for g in range(PASSES):
                 tokens = slice(g * K_PASS, (g + 1) * K_PASS)
-                bank = xz_pass_to_o_layout(xz_rows[batch][:, g, :, place * P : (place + 1) * P])
+                bank = xz_pass_to_o_layout(xz_rows[t][:, g, :, :])
                 nc.vector.scalar_tensor_tensor(
                     out=y[t][:, tokens], in0=beta_all[:, tokens], scalar=neg_kappa[:, t : t + 1],
                     in1=bank[:], op0=ALU.mult, op1=ALU.add,
                 )
-            if place == BATCH - 1 and batch + 2 < BATCHES:
-                xz_rows[batch + 2] = load_token_rows(early, xz, F32, (batch + 2) * BATCH * P, BATCH * P, "xz_rows")
+            if t + XZ_BUFS < O_TILES:
+                xz_rows[t + XZ_BUFS] = load_token_rows(early, xz, F32, (t + XZ_BUFS) * P, P, "xz_rows", XZ_BUFS)
 
         def sign(t):
             half_sign[t] = early.tile([P, TOKENS], BF16, name="half_sign", tag="half_sign", bufs=2 * BATCH)
             nc.vector.tensor_scalar(
-                out=half_sign[t][:], in0=y[t][:], scalar1=0.0, scalar2=0.5, op0=ALU.is_ge, op1=ALU.subtract
+                out=half_sign[t][:], in0=y[t][:], scalar1=0.0, scalar2=0.5, op0=ALU.is_lt, op1=ALU.subtract
             )
+
+        def abs_by_vector(t):
+            return t >= 2 * BATCH and t % 2 == 1
+
+        def absolute(t):
+            if abs_by_vector(t):
+                asinh[t] = early.tile([P, TOKENS], F32, name="asinh", tag="asinh", bufs=3 * BATCH)
+                nc.vector.scalar_tensor_tensor(
+                    out=asinh[t][:], in0=y[t][:], scalar=-1.0, in1=y[t][:], op0=ALU.mult, op1=ALU.max
+                )
 
         def square(t):
             log1p_sq[t] = early.tile([P, TOKENS], F32, name="log1p_sq", tag="log1p_sq", bufs=2 * BATCH)
@@ -114,21 +131,24 @@ def tile_pvfc_v_kernel(tc, x, z, r, bias, xz, beta, grad_out, out):
             engine.tensor_tensor(out=log1p_sq[t][:], in0=y[t][:], in1=y[t][:], op=ALU.mult)
 
         def first_log(t):
-            asinh[t] = early.tile([P, TOKENS], F32, name="asinh", tag="asinh", bufs=3 * BATCH)
-            nc.scalar.activation(out=asinh[t][:], in_=y[t][:], func=ACT.Abs, scale=cz[:, t : t + 1])
+            if not abs_by_vector(t):
+                asinh[t] = early.tile([P, TOKENS], F32, name="asinh", tag="asinh", bufs=3 * BATCH)
+                nc.scalar.activation(out=asinh[t][:], in_=y[t][:], func=ACT.Abs)
             nc.scalar.activation(out=log1p_sq[t][:], in_=log1p_sq[t][:], func=ACT.Ln, scale=cz_sq[:, t : t + 1], bias=one[:])
 
         def root(t):
             root_tile = early.tile([P, TOKENS], F32, name="root", tag="root")
             for cols in pieces(t):
-                nc.scalar.activation(out=root_tile[:, cols], in_=log1p_sq[t][:, cols], func=ACT.Exp, scale=0.5)
+                nc.scalar.activation(
+                    out=root_tile[:, cols], in_=log1p_sq[t][:, cols], func=ACT.Exp, scale=0.5, bias=neg_ln_cz[:, t : t + 1]
+                )
                 for_sbuf_pairs(t).tensor_tensor(
                     out=asinh[t][:, cols], in0=asinh[t][:, cols], in1=root_tile[:, cols], op=ALU.add
                 )
 
         def second_log(t):
             for cols in pieces(t):
-                nc.scalar.activation(out=asinh[t][:, cols], in_=asinh[t][:, cols], func=ACT.Ln)
+                nc.scalar.activation(out=asinh[t][:, cols], in_=asinh[t][:, cols], func=ACT.Ln, scale=cz[:, t : t + 1])
                 for_sbuf_pairs(t).tensor_tensor(
                     out=asinh[t][:, cols], in0=asinh[t][:, cols], in1=half_sign[t][:, cols], op=ALU.mult
                 )
@@ -144,21 +164,25 @@ def tile_pvfc_v_kernel(tc, x, z, r, bias, xz, beta, grad_out, out):
                     out=beta_rows[:, g, 0:PACK],
                     in_=beta[g * K_PASS : (g + 1) * K_PASS, :].rearrange("(q j) one -> q (j one)", j=PACK),
                 )
-            z_all = setup.tile([P, O_TILES, D_MODEL], BF16, bufs=1)
+            z_all = setup.tile([P, 4 * BATCH, D_MODEL], BF16, bufs=1)
             z_tiles = z.rearrange("(t p) d -> p t d", p=P)
 
             def load_z(first, count):
                 nc.sync.dma_start(out=z_all[:, first : first + count, :], in_=z_tiles[:, first : first + count, :])
 
-            for batch in range(2):
-                load_z(batch * BATCH, BATCH)
-                xz_rows[batch] = load_token_rows(early, xz, F32, batch * BATCH * P, BATCH * P, "xz_rows")
-            for first in range(2 * BATCH, O_TILES, 4):
-                load_z(first, 4)
+            for t in range(XZ_BUFS):
+                if t % BATCH == 0:
+                    load_z(t, BATCH)
+                xz_rows[t] = load_token_rows(early, xz, F32, t * P, P, "xz_rows", XZ_BUFS)
+            load_z(2 * BATCH, 2 * BATCH)
             x_raw = {}
-            for g in range(PASSES):
-                x_raw[g] = setup.tile([P, PACK, D_MODEL], BF16, name="x_raw", tag="x_raw", bufs=PASSES)
+
+            def load_x(g):
+                x_raw[g] = setup.tile([P, PACK, D_MODEL], BF16, name="x_raw", tag="x_raw")
                 nc.sync.dma_start(out=x_raw[g][:], in_=pass_rows(x, g, 0, D_MODEL))
+
+            for g in range(2):
+                load_x(g)
 
             vector_cols = psum.tile([P, P], BF16, tag="feed")
             nc.tensor.transpose(vector_cols[:], vector_rows[:], ident_bf16[:])
@@ -177,10 +201,8 @@ def tile_pvfc_v_kernel(tc, x, z, r, bias, xz, beta, grad_out, out):
             nc.vector.tensor_tensor(out=two_cosh_r[:], in0=exp_r[:], in1=exp_neg_r[:], op=ALU.add)
             cosh_r = per_feature("cosh_r")
             nc.vector.tensor_scalar_mul(out=cosh_r[:], in0=two_cosh_r[:], scalar1=0.5)
-            half_cosh_r = per_feature("half_cosh_r")
-            nc.vector.tensor_scalar_mul(out=half_cosh_r[:], in0=two_cosh_r[:], scalar1=0.25)
-            neg_bias = per_feature("neg_bias")
-            nc.vector.tensor_scalar_mul(out=neg_bias[:], in0=bias_col, scalar1=-1.0)
+            inv_cosh_r = per_feature("inv_cosh_r")
+            nc.vector.reciprocal(out=inv_cosh_r[:], in_=cosh_r[:])
 
             beta_all = keep.tile([P, TOKENS], F32)
             for g in range(PASSES):
@@ -209,6 +231,7 @@ def tile_pvfc_v_kernel(tc, x, z, r, bias, xz, beta, grad_out, out):
                     (neg_kappa, zn, neg_tanh_r, ALU.mult),
                     (cz, cosh_r, inv_zn, ALU.mult),
                     (cz_sq, cz, cz, ALU.mult),
+                    (inv_cz, zn, inv_cosh_r, ALU.mult),
                     (two_zn, zn, zn, ALU.add),
                     (neg_two_zn, zn, minus_two, ALU.mult),
                     (neg_inv_zn, inv_zn, minus_one, ALU.mult),
@@ -216,7 +239,14 @@ def tile_pvfc_v_kernel(tc, x, z, r, bias, xz, beta, grad_out, out):
                 ):
                     engine.tensor_tensor(out=result[:, ts], in0=a[:, ts], in1=b[:, ts], op=op)
 
-            next_tiles, other_tiles = slice(2 * BATCH, 4 * BATCH), slice(4 * BATCH, O_TILES)
+            def exponent_biases(ts, engine):
+                nc.scalar.activation(out=ln_zn[:, ts], in_=zn[:, ts], func=ACT.Ln)
+                nc.scalar.activation(out=ln_half_cz[:, ts], in_=cz[:, ts], func=ACT.Ln, scale=0.5)
+                nc.scalar.activation(out=neg_ln_cz[:, ts], in_=inv_cz[:, ts], func=ACT.Ln)
+                engine.tensor_tensor(out=bias_v[:, ts], in0=ln_zn[:, ts], in1=bias_col[:, ts], op=ALU.add)
+                engine.tensor_tensor(out=bias_neg_v[:, ts], in0=ln_zn[:, ts], in1=bias_col[:, ts], op=ALU.subtract)
+
+            first_tiles, next_tiles, other_tiles = slice(0, 2 * BATCH), slice(2 * BATCH, 4 * BATCH), slice(4 * BATCH, O_TILES)
             for t in range(BATCH):
                 square_norm_on_vector(t)
             feature_quantities(slice(0, BATCH), nc.vector)
@@ -227,6 +257,7 @@ def tile_pvfc_v_kernel(tc, x, z, r, bias, xz, beta, grad_out, out):
                 square(t)
                 first_log(t)
             feature_quantities(slice(BATCH, 2 * BATCH), nc.vector)
+            exponent_biases(first_tiles, nc.vector)
             for t in range(BATCH):
                 sign(t)
             for t in range(2 * BATCH, 4 * BATCH):
@@ -242,9 +273,8 @@ def tile_pvfc_v_kernel(tc, x, z, r, bias, xz, beta, grad_out, out):
             second_log(1)
             for t in range(BATCH, 2 * BATCH):
                 sign(t)
+                absolute(t)
                 first_log(t)
-            for t in range(4 * BATCH, O_TILES):
-                square_norm_on_scalar(t)
 
             x_codes = keep.tile([P, PASSES, D_MODEL], U32, align_bytes=64)
             x_scales = keep.tile([P, PASSES, D_MODEL], U8, align_bytes=64)
@@ -256,6 +286,8 @@ def tile_pvfc_v_kernel(tc, x, z, r, bias, xz, beta, grad_out, out):
                         out=x_grouped[g][:].rearrange("p (c i) j -> p c j i", i=4),
                         in_=x_raw[g][:].rearrange("p j (c i) -> p c j i", i=4),
                     )
+                    if g + 2 < PASSES:
+                        load_x(g + 2)
                 if g > 0:
                     nc.vector.quantize_mx(
                         out=x_codes[:, g - 1, :].bitcast(E4M3_X4),
@@ -264,10 +296,22 @@ def tile_pvfc_v_kernel(tc, x, z, r, bias, xz, beta, grad_out, out):
                     )
 
         late = stack.enter_context(tc.tile_pool(name="late", bufs=2, reuse_waits="tile"))
-        inv_root, exp_v, exp_neg_v, dxz, back_banks, grouped, dxz_codes, dxz_scales = {}, {}, {}, {}, {}, {}, {}, {}
-        g_rows, xz_again, z_tile, dv2_rows = {}, {}, {}, {}
-        t_parts = keep.tile([P, O_TILES, 2 * PASSES], F32)
+        inv_root, exp_v, exp_neg_v, u_xz, dv2, grouped, dxz_codes, dxz_scales, sums = {}, {}, {}, {}, {}, {}, {}, {}, {}
+        g_rows, xz_again, z_tile, late_rows = {}, {}, {}, {}
         t_over_zn = keep.tile([P, O_TILES], F32)
+
+        def load_late_rows(t):
+            if t < O_TILES:
+                tag = "result" if t % 2 == 0 else "z_tile"
+                late_rows[t] = late.tile([P, D_MODEL], BF16, name="late_rows", tag=tag, bufs=LATE_ROWS // 2)
+                nc.sync.dma_start(out=late_rows[t][:], in_=z[t * P : (t + 1) * P, :])
+
+        def late_square_norm(t):
+            rows = late_rows[t]
+            nc.scalar.activation(out=rows[:], in_=rows[:], func=ACT.Square, accum_out=zn_sq[:, t : t + 1])
+
+        for t in range(4 * BATCH, 4 * BATCH + LATE_ROWS):
+            load_late_rows(t)
 
         def load_g_rows(batch):
             if batch < BATCHES:
@@ -282,98 +326,91 @@ def tile_pvfc_v_kernel(tc, x, z, r, bias, xz, beta, grad_out, out):
                 z_tile[t] = late.tile([P, D_MODEL], BF16, name="z_tile", tag="z_tile", bufs=Z_BUFS)
                 nc.sync.dma_start(out=z_tile[t][:], in_=z[t * P : (t + 1) * P, :])
 
-        Z_BUFS = BATCH + 1
         for first_two in range(2):
             load_g_rows(first_two)
             load_xz_again(first_two)
-        for t in range(Z_BUFS):
-            load_z_tile(t)
 
         def exponentials(t):
-            exp_v[t] = late.tile([P, TOKENS], F32, name="exp_v", tag="exp_v")
-            nc.scalar.activation(
-                out=exp_v[t][:], in_=asinh[t][:], func=ACT.Exp, scale=two_zn[:, t : t + 1], bias=bias_col[:, t : t + 1]
-            )
-            exp_neg_v[t] = late.tile([P, TOKENS], F32, name="exp_neg_v", tag="exp_neg_v")
-            nc.scalar.activation(
-                out=exp_neg_v[t][:], in_=asinh[t][:], func=ACT.Exp,
-                scale=neg_two_zn[:, t : t + 1], bias=neg_bias[:, t : t + 1],
-            )
-            inv_root[t] = late.tile([P, TOKENS], F32, name="inv_root", tag="inv_root")
-            nc.scalar.activation(out=inv_root[t][:], in_=log1p_sq[t][:], func=ACT.Exp, scale=-0.5)
+            inv_root[t] = early.tile([P, TOKENS], F32, name="inv_root", tag="inv_root")
+            exp_v[t] = early.tile([P, TOKENS], F32, name="exp_v", tag="exp_v")
+            exp_neg_v[t] = early.tile([P, TOKENS], F32, name="exp_neg_v", tag="exp_neg_v")
+            for cols in pieces(t):
+                nc.scalar.activation(
+                    out=inv_root[t][:, cols], in_=log1p_sq[t][:, cols], func=ACT.Exp, scale=-0.5,
+                    bias=ln_half_cz[:, t : t + 1],
+                )
+                nc.scalar.activation(
+                    out=exp_v[t][:, cols], in_=asinh[t][:, cols], func=ACT.Exp,
+                    scale=neg_two_zn[:, t : t + 1], bias=bias_v[:, t : t + 1],
+                )
+                nc.scalar.activation(
+                    out=exp_neg_v[t][:, cols], in_=asinh[t][:, cols], func=ACT.Exp,
+                    scale=two_zn[:, t : t + 1], bias=bias_neg_v[:, t : t + 1],
+                )
 
-        def grad_v(t):
+        def to_token_layout(tiles, g):
+            bank = psum.tile([P, PACK, P], F32, name="token_bank", tag="feed")
+            for j in range(PACK):
+                first = (g * PACK + j) * P
+                for i, tile in enumerate(tiles):
+                    nc.tensor.matmul(
+                        out=bank[:, j, :], lhsT=tile[:, first : first + P], rhs=ident_f32[:], is_transpose=True,
+                        start=(i == 0), stop=(i == len(tiles) - 1),
+                    )
+            return bank
+
+        def start_gradients(t):
             batch, place = divmod(t, BATCH)
-            dv2_rows[t] = late.tile([P, PASSES, PACK, P], F32, name="dv2_rows", tag="dv2_rows", bufs=1)
+            u_xz[t] = late.tile([P, TOKENS], F32, name="u_xz", tag="u_xz", bufs=1)
             for g in range(PASSES):
-                bank = psum.tile([P, K_PASS], F32, name="cosh_bank", tag="feed")
-                for j in range(PACK):
-                    block = slice((g * PACK + j) * P, (g * PACK + j + 1) * P)
-                    nc.tensor.matmul(
-                        out=bank[:, j * P : (j + 1) * P], lhsT=exp_v[t][:, block], rhs=ident_f32[:],
-                        is_transpose=True, start=True, stop=False,
-                    )
-                    nc.tensor.matmul(
-                        out=bank[:, j * P : (j + 1) * P], lhsT=exp_neg_v[t][:, block], rhs=ident_f32[:],
-                        is_transpose=True, start=False, stop=True,
-                    )
+                tokens = slice(g * K_PASS, (g + 1) * K_PASS)
+                bank = xz_pass_to_o_layout(xz_again[t][:, g, :, :])
+                nc.vector.tensor_tensor(out=u_xz[t][:, tokens], in0=inv_root[t][:, tokens], in1=bank[:], op=ALU.mult)
+            load_xz_again(t + 2)
+            if t > 0:
+                sum_over_groups(t - 1)
+            dv2[t] = late.tile([P, PASSES, PACK, P], F32, name="dv2", tag="dv2", bufs=1)
+            for g in range(PASSES):
+                bank = to_token_layout([exp_v[t], exp_neg_v[t]], g)
                 nc.vector.tensor_tensor(
-                    out=dv2_rows[t][:, g, :, :], in0=g_rows[batch][:, g, :, place * P : (place + 1) * P],
-                    in1=bank[:].rearrange("p (j o) -> p j o", j=PACK), op=ALU.mult,
+                    out=dv2[t][:, g, :, :], in0=g_rows[batch][:, g, :, place * P : (place + 1) * P], in1=bank[:], op=ALU.mult
                 )
             if place == BATCH - 1:
                 load_g_rows(batch + 2)
 
-        def grad_xz(t):
-            dxz[t] = late.tile([P, TOKENS], F32, name="dxz", tag="dxz", bufs=1)
-            for g in range(PASSES):
-                tokens = slice(g * K_PASS, (g + 1) * K_PASS)
-                bank = psum.tile([P, K_PASS], F32, name="dv2_bank", tag="feed")
-                for j in range(PACK):
-                    nc.tensor.transpose(bank[:, j * P : (j + 1) * P], dv2_rows[t][:, g, j, :], ident_f32[:])
-                nc.vector.scalar_tensor_tensor(
-                    out=dxz[t][:, tokens], in0=bank[:], scalar=half_cosh_r[:, t : t + 1], in1=inv_root[t][:, tokens],
-                    op0=ALU.mult, op1=ALU.mult,
+        def end_gradients(t):
+            grouped[t] = late.tile([P, PASSES, P, PACK], BF16, name="grouped", tag="grouped", align_bytes=64)
+
+            def times_u(g):
+                bank = to_token_layout([inv_root[t]], g)
+                nc.vector.tensor_tensor(
+                    out=grouped[t][:, g, :, :].rearrange("p (c i) j -> p c j i", i=4),
+                    in0=dv2[t][:, g, :, :].rearrange("p j (c i) -> p c j i", i=4),
+                    in1=bank[:].rearrange("p j (c i) -> p c j i", i=4), op=ALU.mult,
                 )
-                products = late.tile([P, K_PASS], BF16, name="products", tag="products")
-                nc.vector.scalar_tensor_tensor(
-                    out=products[:], in0=bank[:], scalar=inv_zn[:, t : t + 1], in1=asinh[t][:, tokens],
-                    op0=ALU.mult, op1=ALU.mult, accum_out=t_parts[:, t, g : g + 1],
+
+            def times_bracket(g):
+                bank = to_token_layout([asinh[t], u_xz[t]], g)
+                nc.vector.tensor_tensor(out=dv2[t][:, g, :, :], in0=dv2[t][:, g, :, :], in1=bank[:], op=ALU.mult)
+
+            times_u(0)
+            times_u(1)
+            times_bracket(0)
+            times_u(2)
+            times_bracket(1)
+            times_bracket(2)
+
+        def sum_over_groups(t):
+            sums[t] = psum.tile([P, P], F32, name="sums", tag="sums", bufs=1)
+            blocks = [(g, j) for g in range(PASSES) for j in range(PACK)]
+            for g, j in blocks:
+                nc.tensor.matmul(
+                    out=sums[t][:], lhsT=dv2[t][:, g, j, :], rhs=ident_f32[:], is_transpose=True,
+                    start=((g, j) == blocks[0]), stop=((g, j) == blocks[-1]),
                 )
-            for g in range(PASSES):
-                tokens = slice(g * K_PASS, (g + 1) * K_PASS)
-                bank = xz_pass_to_o_layout(xz_again[t][:, g, :, :])
-                products = late.tile([P, K_PASS], BF16, name="products", tag="products")
-                nc.vector.scalar_tensor_tensor(
-                    out=products[:], in0=dxz[t][:, tokens], scalar=neg_inv_zn_sq[:, t : t + 1], in1=bank[:],
-                    op0=ALU.mult, op1=ALU.mult, accum_out=t_parts[:, t, PASSES + g : PASSES + g + 1],
-                )
-            load_xz_again(t + 2)
-            back_banks[t] = []
-            for g in range(PASSES):
-                bank = psum.tile([P, K_PASS], F32, name="back_bank", tag="back")
-                for j in range(PACK):
-                    first = (g * PACK + j) * P
-                    nc.tensor.transpose(bank[:, j * P : (j + 1) * P], dxz[t][:, first : first + P], ident_f32[:])
-                back_banks[t].append(bank)
 
-        def banks_emptied_by_scalar(t):
-            return 0 if t < O_TILES - BATCH else PASSES
-
-        def group_dxz(t, g, copy):
-            copy(out=grouped[t][:, g, :, :], in_=back_banks[t][g][:].rearrange("p (j o) -> p o j", j=PACK))
-
-        def group_on_vector(t):
-            grouped[t] = late.tile([P, PASSES, P, PACK], BF16, name="dxz_grouped", tag="dxz_grouped", align_bytes=64)
-            for g in range(banks_emptied_by_scalar(t), PASSES):
-                group_dxz(t, g, nc.vector.tensor_copy)
-            nc.vector.tensor_reduce(
-                out=t_over_zn[:, t : t + 1], in_=t_parts[:, t, :], axis=mybir.AxisListType.X, op=ALU.add
-            )
-
-        def group_on_scalar(t):
-            for g in range(banks_emptied_by_scalar(t)):
-                group_dxz(t, g, nc.scalar.copy)
+        def sum_over_tokens(t):
+            nc.vector.tensor_reduce(out=t_sum[:, t : t + 1], in_=sums[t][:], axis=mybir.AxisListType.X, op=ALU.add)
 
         def quantise_dxz(t):
             dxz_codes[t] = late.tile([P, PASSES, P], U32, name="dxz_codes", tag="dxz_codes", align_bytes=64)
@@ -386,9 +423,12 @@ def tile_pvfc_v_kernel(tc, x, z, r, bias, xz, beta, grad_out, out):
                 )
 
         def finish(t):
+            nc.vector.tensor_scalar_mul(
+                out=t_over_zn[:, t : t + 1], in0=t_sum[:, t : t + 1], scalar1=neg_inv_zn_sq[:, t : t + 1]
+            )
             for n in range(D_HALVES):
                 cols = slice(n * N_TILE, (n + 1) * N_TILE)
-                product = psum.tile([P, N_TILE], F32, name="product", tag="back")
+                product = psum.tile([P, N_TILE], F32, name="product", tag="product", bufs=2)
                 for g in range(PASSES):
                     nc.tensor.matmul_mx(
                         out=product[:],
@@ -399,7 +439,7 @@ def tile_pvfc_v_kernel(tc, x, z, r, bias, xz, beta, grad_out, out):
                         start=(g == 0),
                         stop=(g == PASSES - 1),
                     )
-                result = late.tile([P, N_TILE], F32, name="result", tag="result", bufs=3)
+                result = late.tile([P, N_TILE], F32, name="result", tag="result", bufs=LATE_ROWS // 2)
                 nc.vector.scalar_tensor_tensor(
                     out=result[:], in0=z_tile[t][:, cols], scalar=t_over_zn[:, t : t + 1], in1=product[:],
                     op0=ALU.mult, op1=ALU.add,
@@ -413,33 +453,44 @@ def tile_pvfc_v_kernel(tc, x, z, r, bias, xz, beta, grad_out, out):
 
         for k in range(BATCHES + 2):
             t = BATCH * k
-            run(grad_v, t - 2)
+            run(start_gradients, t - 2)
             run(finish, t - 4)
-            run(grad_xz, t - 2)
-            run(group_on_vector, t - 2)
+            if t - 3 == O_TILES - 1:
+                sum_over_groups(O_TILES - 1)
+            run(sum_over_tokens, t - 3)
+            run(end_gradients, t - 2)
             if k > 0:
                 run(second_log, t)
                 run(second_log, t + 1)
             if k == 1:
+                exponent_biases(next_tiles, nc.gpsimd)
                 feature_quantities(other_tiles, nc.gpsimd)
+            if k == 2:
+                exponent_biases(other_tiles, nc.gpsimd)
             if k > 0:
                 run(first_log, t + 2)
                 run(first_log, t + 3)
-            run(group_on_scalar, t - 2)
+            run(start_gradients, t - 1)
             run(shifted_xz, t + 4)
             run(shifted_xz, t + 5)
-            run(grad_v, t - 1)
             run(quantise_dxz, t - 3)
             run(quantise_dxz, t - 2)
             run(sign, t + 4)
             run(sign, t + 5)
+            run(absolute, t + 4)
+            run(absolute, t + 5)
             run(exponentials, t)
             run(root, t + 2)
             run(root, t + 3)
             run(square, t + 4)
             run(finish, t - 3)
-            run(grad_xz, t - 1)
-            run(group_on_vector, t - 1)
+            run(sum_over_tokens, t - 2)
+            run(end_gradients, t - 1)
             run(exponentials, t + 1)
-            run(group_on_scalar, t - 1)
             run(square, t + 5)
+            if k == 0:
+                for late_tile in range(4 * BATCH, O_TILES):
+                    late_square_norm(late_tile)
+                    load_late_rows(late_tile + LATE_ROWS)
+                for first in range(Z_BUFS):
+                    load_z_tile(first)

from contextlib import ExitStack

import concourse.mybir as mybir
from concourse.masks import make_identity

F32 = mybir.dt.float32
BF16 = mybir.dt.bfloat16
U32 = mybir.dt.uint32
U8 = mybir.dt.uint8
E4M3_X4 = mybir.dt.float8_e4m3fn_x4
E5M2_X4 = mybir.dt.float8_e5m2_x4
ACT = mybir.ActivationFunctionType
ALU = mybir.AluOpType

TOKENS, D_MODEL, OUT_FEATURES = 1536, 1024, 2048
FLOPS = 2 * TOKENS * D_MODEL * OUT_FEATURES

P = 128
PACK = 4
K_PASS = P * PACK
PASSES = TOKENS // K_PASS
O_TILES = OUT_FEATURES // P
BATCH = 2
BATCHES = O_TILES // BATCH
N_TILE = 512
D_HALVES = D_MODEL // N_TILE
XZ_BUFS = 3
Z_BUFS = BATCH + 1
LATE_ROWS = 6


def tile_pvfc_v_kernel(tc, x, z, r, bias, xz, beta, grad_out, out):
    nc = tc.nc

    def pass_rows(matrix, g, first_col, width):
        rows = matrix[g * K_PASS : (g + 1) * K_PASS, first_col : first_col + width]
        return rows.rearrange("(q j) c -> q j c", j=PACK)

    def load_token_rows(pool, matrix, dtype, first_col, width, name, bufs=2):
        rows = pool.tile([P, PASSES, PACK, width], dtype, name=name, tag=name, bufs=bufs)
        for g in range(PASSES):
            nc.sync.dma_start(out=rows[:, g, :, :], in_=pass_rows(matrix, g, first_col, width))
        return rows

    with ExitStack() as stack:
        stack.enter_context(tc.manual_schedule())
        keep = stack.enter_context(tc.tile_pool(name="keep", bufs=1))
        early = stack.enter_context(tc.tile_pool(name="early", bufs=2))
        psum = stack.enter_context(tc.psum_pool(name="psum", bufs=5))

        ident_f32 = keep.tile([P, P], F32)
        make_identity(nc, ident_f32[:])
        ident_bf16 = keep.tile([P, P], BF16)
        make_identity(nc, ident_bf16[:])
        one = keep.tile([P, 1], F32)
        nc.vector.memset(one[:], 1.0)

        def per_feature(name):
            return keep.tile([P, O_TILES], F32, name=name, tag=name)

        def constant(name, value):
            tile = per_feature(name)
            nc.vector.memset(tile[:], value)
            return tile

        half, minus_half, minus_one, minus_two = [
            constant(name, value)
            for name, value in (("half", 0.5), ("minus_half", -0.5), ("minus_one", -1.0), ("minus_two", -2.0))
        ]
        zn_sq, zn, inv_zn, neg_inv_zn, neg_inv_zn_sq, two_zn, neg_two_zn = [
            per_feature(name)
            for name in ("zn_sq", "zn", "inv_zn", "neg_inv_zn", "neg_inv_zn_sq", "two_zn", "neg_two_zn")
        ]
        ln_zn, ln_half_cz, bias_v, bias_neg_v, t_sum = [
            per_feature(name) for name in ("ln_zn", "ln_half_cz", "bias_v", "bias_neg_v", "t_sum")
        ]
        neg_kappa, cz, cz_sq, inv_cz, neg_ln_cz = [
            per_feature(name) for name in ("neg_kappa", "cz", "cz_sq", "inv_cz", "neg_ln_cz")
        ]

        xz_rows, y, log1p_sq, asinh, half_sign = {}, {}, {}, {}, {}

        def xz_pass_to_o_layout(block):
            bank = psum.tile([P, K_PASS], F32, name="xz_bank", tag="feed")
            for j in range(PACK):
                nc.tensor.transpose(bank[:, j * P : (j + 1) * P], block[:, j, :], ident_f32[:])
            return bank

        def fills_the_pipeline(t):
            return t < BATCH

        def pieces(t):
            if BATCH <= t < O_TILES - BATCH:
                return [slice(0, TOKENS)]
            return [slice(g * K_PASS, (g + 1) * K_PASS) for g in range(PASSES)]

        def for_sbuf_pairs(t):
            return nc.vector if fills_the_pipeline(t) else nc.gpsimd

        def shifted_xz(t):
            y[t] = early.tile([P, TOKENS], F32, name="y", tag="y", bufs=XZ_BUFS)
            for g in range(PASSES):
                tokens = slice(g * K_PASS, (g + 1) * K_PASS)
                bank = xz_pass_to_o_layout(xz_rows[t][:, g, :, :])
                nc.vector.scalar_tensor_tensor(
                    out=y[t][:, tokens], in0=beta_all[:, tokens], scalar=neg_kappa[:, t : t + 1],
                    in1=bank[:], op0=ALU.mult, op1=ALU.add,
                )
            if t + XZ_BUFS < O_TILES:
                xz_rows[t + XZ_BUFS] = load_token_rows(early, xz, F32, (t + XZ_BUFS) * P, P, "xz_rows", XZ_BUFS)

        def sign(t):
            half_sign[t] = early.tile([P, TOKENS], BF16, name="half_sign", tag="half_sign", bufs=2 * BATCH)
            nc.vector.tensor_scalar(
                out=half_sign[t][:], in0=y[t][:], scalar1=0.0, scalar2=0.5, op0=ALU.is_lt, op1=ALU.subtract
            )

        def abs_by_vector(t):
            return t >= 2 * BATCH and t % 2 == 1

        def absolute(t):
            if abs_by_vector(t):
                asinh[t] = early.tile([P, TOKENS], F32, name="asinh", tag="asinh", bufs=3 * BATCH)
                nc.vector.scalar_tensor_tensor(
                    out=asinh[t][:], in0=y[t][:], scalar=-1.0, in1=y[t][:], op0=ALU.mult, op1=ALU.max
                )

        def square(t):
            log1p_sq[t] = early.tile([P, TOKENS], F32, name="log1p_sq", tag="log1p_sq", bufs=2 * BATCH)
            engine = nc.vector if t < 2 * BATCH else nc.gpsimd
            engine.tensor_tensor(out=log1p_sq[t][:], in0=y[t][:], in1=y[t][:], op=ALU.mult)

        def first_log(t):
            if not abs_by_vector(t):
                asinh[t] = early.tile([P, TOKENS], F32, name="asinh", tag="asinh", bufs=3 * BATCH)
                nc.scalar.activation(out=asinh[t][:], in_=y[t][:], func=ACT.Abs)
            nc.scalar.activation(out=log1p_sq[t][:], in_=log1p_sq[t][:], func=ACT.Ln, scale=cz_sq[:, t : t + 1], bias=one[:])

        def root(t):
            root_tile = early.tile([P, TOKENS], F32, name="root", tag="root")
            for cols in pieces(t):
                nc.scalar.activation(
                    out=root_tile[:, cols], in_=log1p_sq[t][:, cols], func=ACT.Exp, scale=0.5, bias=neg_ln_cz[:, t : t + 1]
                )
                for_sbuf_pairs(t).tensor_tensor(
                    out=asinh[t][:, cols], in0=asinh[t][:, cols], in1=root_tile[:, cols], op=ALU.add
                )

        def second_log(t):
            for cols in pieces(t):
                nc.scalar.activation(out=asinh[t][:, cols], in_=asinh[t][:, cols], func=ACT.Ln, scale=cz[:, t : t + 1])
                for_sbuf_pairs(t).tensor_tensor(
                    out=asinh[t][:, cols], in0=asinh[t][:, cols], in1=half_sign[t][:, cols], op=ALU.mult
                )

        with tc.tile_pool(name="setup", bufs=2) as setup:
            vector_rows = setup.tile([P, P], BF16, bufs=1)
            nc.vector.memset(vector_rows[:], 0.0)
            nc.sync.dma_start(out=vector_rows[0:O_TILES, :], in_=r.rearrange("(t p) one -> t (p one)", p=P))
            nc.sync.dma_start(out=vector_rows[O_TILES : 2 * O_TILES, :], in_=bias.rearrange("(t p) -> t p", p=P))
            beta_rows = setup.tile([P, PASSES, 2 * PACK], F32, bufs=1)
            for g in range(PASSES):
                nc.sync.dma_start(
                    out=beta_rows[:, g, 0:PACK],
                    in_=beta[g * K_PASS : (g + 1) * K_PASS, :].rearrange("(q j) one -> q (j one)", j=PACK),
                )
            z_all = setup.tile([P, 4 * BATCH, D_MODEL], BF16, bufs=1)
            z_tiles = z.rearrange("(t p) d -> p t d", p=P)

            def load_z(first, count):
                nc.sync.dma_start(out=z_all[:, first : first + count, :], in_=z_tiles[:, first : first + count, :])

            for t in range(XZ_BUFS):
                if t % BATCH == 0:
                    load_z(t, BATCH)
                xz_rows[t] = load_token_rows(early, xz, F32, t * P, P, "xz_rows", XZ_BUFS)
            load_z(2 * BATCH, 2 * BATCH)
            x_raw = {}

            def load_x(g):
                x_raw[g] = setup.tile([P, PACK, D_MODEL], BF16, name="x_raw", tag="x_raw")
                nc.sync.dma_start(out=x_raw[g][:], in_=pass_rows(x, g, 0, D_MODEL))

            for g in range(2):
                load_x(g)

            vector_cols = psum.tile([P, P], BF16, tag="feed")
            nc.tensor.transpose(vector_cols[:], vector_rows[:], ident_bf16[:])
            r_and_bias = keep.tile([P, 2 * O_TILES], F32)
            nc.vector.tensor_copy(out=r_and_bias[:], in_=vector_cols[:, 0 : 2 * O_TILES])
            r_col = r_and_bias[:, 0:O_TILES]
            bias_col = r_and_bias[:, O_TILES : 2 * O_TILES]

            exp_r = per_feature("exp_r")
            nc.scalar.activation(out=exp_r[:], in_=r_col, func=ACT.Exp)
            exp_neg_r = per_feature("exp_neg_r")
            nc.scalar.activation(out=exp_neg_r[:], in_=r_col, func=ACT.Exp, scale=-1.0)
            neg_tanh_r = per_feature("neg_tanh_r")
            nc.scalar.activation(out=neg_tanh_r[:], in_=r_col, func=ACT.Tanh, scale=-1.0)
            two_cosh_r = per_feature("two_cosh_r")
            nc.vector.tensor_tensor(out=two_cosh_r[:], in0=exp_r[:], in1=exp_neg_r[:], op=ALU.add)
            cosh_r = per_feature("cosh_r")
            nc.vector.tensor_scalar_mul(out=cosh_r[:], in0=two_cosh_r[:], scalar1=0.5)
            inv_cosh_r = per_feature("inv_cosh_r")
            nc.vector.reciprocal(out=inv_cosh_r[:], in_=cosh_r[:])

            beta_all = keep.tile([P, TOKENS], F32)
            for g in range(PASSES):
                bank = psum.tile([P, K_PASS], F32, name="beta_bank", tag="feed")
                for j in range(PACK):
                    nc.tensor.transpose(
                        bank[:, j * P : (j + 1) * P], beta_rows[:, g, j : j + 1].to_broadcast([P, P]), ident_f32[:]
                    )
                nc.vector.tensor_copy(out=beta_all[:, g * K_PASS : (g + 1) * K_PASS], in_=bank[:])

            def square_norm_on_vector(t):
                squares = setup.tile([P, D_MODEL], BF16, name="squares_v", tag="squares_v")
                nc.vector.scalar_tensor_tensor(
                    out=squares[:], in0=z_all[:, t, :], scalar=1.0, in1=z_all[:, t, :],
                    op0=ALU.mult, op1=ALU.mult, accum_out=zn_sq[:, t : t + 1],
                )

            def square_norm_on_scalar(t):
                squares = setup.tile([P, D_MODEL], BF16, name="squares_s", tag="squares_s")
                nc.scalar.activation(out=squares[:], in_=z_all[:, t, :], func=ACT.Square, accum_out=zn_sq[:, t : t + 1])

            def feature_quantities(ts, engine):
                nc.gpsimd.tensor_tensor(out=zn[:, ts], in0=zn_sq[:, ts], in1=half[:, ts], op=ALU.pow)
                nc.gpsimd.tensor_tensor(out=inv_zn[:, ts], in0=zn_sq[:, ts], in1=minus_half[:, ts], op=ALU.pow)
                for result, a, b, op in (
                    (neg_kappa, zn, neg_tanh_r, ALU.mult),
                    (cz, cosh_r, inv_zn, ALU.mult),
                    (cz_sq, cz, cz, ALU.mult),
                    (inv_cz, zn, inv_cosh_r, ALU.mult),
                    (two_zn, zn, zn, ALU.add),
                    (neg_two_zn, zn, minus_two, ALU.mult),
                    (neg_inv_zn, inv_zn, minus_one, ALU.mult),
                    (neg_inv_zn_sq, neg_inv_zn, inv_zn, ALU.mult),
                ):
                    engine.tensor_tensor(out=result[:, ts], in0=a[:, ts], in1=b[:, ts], op=op)

            def exponent_biases(ts, engine):
                nc.scalar.activation(out=ln_zn[:, ts], in_=zn[:, ts], func=ACT.Ln)
                nc.scalar.activation(out=ln_half_cz[:, ts], in_=cz[:, ts], func=ACT.Ln, scale=0.5)
                nc.scalar.activation(out=neg_ln_cz[:, ts], in_=inv_cz[:, ts], func=ACT.Ln)
                engine.tensor_tensor(out=bias_v[:, ts], in0=ln_zn[:, ts], in1=bias_col[:, ts], op=ALU.add)
                engine.tensor_tensor(out=bias_neg_v[:, ts], in0=ln_zn[:, ts], in1=bias_col[:, ts], op=ALU.subtract)

            first_tiles, next_tiles, other_tiles = slice(0, 2 * BATCH), slice(2 * BATCH, 4 * BATCH), slice(4 * BATCH, O_TILES)
            for t in range(BATCH):
                square_norm_on_vector(t)
            feature_quantities(slice(0, BATCH), nc.vector)
            for t in range(BATCH, 2 * BATCH):
                square_norm_on_scalar(t)
            for t in range(BATCH):
                shifted_xz(t)
                square(t)
                first_log(t)
            feature_quantities(slice(BATCH, 2 * BATCH), nc.vector)
            exponent_biases(first_tiles, nc.vector)
            for t in range(BATCH):
                sign(t)
            for t in range(2 * BATCH, 4 * BATCH):
                square_norm_on_vector(t)
            for t in range(BATCH):
                root(t)
            feature_quantities(next_tiles, nc.gpsimd)
            shifted_xz(BATCH)
            square(BATCH)
            second_log(0)
            shifted_xz(BATCH + 1)
            square(BATCH + 1)
            second_log(1)
            for t in range(BATCH, 2 * BATCH):
                sign(t)
                absolute(t)
                first_log(t)

            x_codes = keep.tile([P, PASSES, D_MODEL], U32, align_bytes=64)
            x_scales = keep.tile([P, PASSES, D_MODEL], U8, align_bytes=64)
            x_grouped = {}
            for g in range(PASSES + 1):
                if g < PASSES:
                    x_grouped[g] = setup.tile([P, D_MODEL, PACK], BF16, name="x_grouped", tag="x_grouped", align_bytes=64)
                    nc.vector.tensor_copy(
                        out=x_grouped[g][:].rearrange("p (c i) j -> p c j i", i=4),
                        in_=x_raw[g][:].rearrange("p j (c i) -> p c j i", i=4),
                    )
                    if g + 2 < PASSES:
                        load_x(g + 2)
                if g > 0:
                    nc.vector.quantize_mx(
                        out=x_codes[:, g - 1, :].bitcast(E4M3_X4),
                        scales=x_scales[:, g - 1, :],
                        in_=x_grouped[g - 1][:].rearrange("p d j -> p (d j)"),
                    )

        late = stack.enter_context(tc.tile_pool(name="late", bufs=2, reuse_waits="tile"))
        inv_root, exp_v, exp_neg_v, u_xz, dv2, grouped, dxz_codes, dxz_scales, sums = {}, {}, {}, {}, {}, {}, {}, {}, {}
        g_rows, xz_again, z_tile, late_rows = {}, {}, {}, {}
        t_over_zn = keep.tile([P, O_TILES], F32)

        def load_late_rows(t):
            if t < O_TILES:
                tag = "result" if t % 2 == 0 else "z_tile"
                late_rows[t] = late.tile([P, D_MODEL], BF16, name="late_rows", tag=tag, bufs=LATE_ROWS // 2)
                nc.sync.dma_start(out=late_rows[t][:], in_=z[t * P : (t + 1) * P, :])

        def late_square_norm(t):
            rows = late_rows[t]
            nc.scalar.activation(out=rows[:], in_=rows[:], func=ACT.Square, accum_out=zn_sq[:, t : t + 1])

        for t in range(4 * BATCH, 4 * BATCH + LATE_ROWS):
            load_late_rows(t)

        def load_g_rows(batch):
            if batch < BATCHES:
                g_rows[batch] = load_token_rows(late, grad_out, BF16, batch * BATCH * P, BATCH * P, "g_rows")

        def load_xz_again(t):
            if t < O_TILES:
                xz_again[t] = load_token_rows(late, xz, F32, t * P, P, "xz_again")

        def load_z_tile(t):
            if t < O_TILES:
                z_tile[t] = late.tile([P, D_MODEL], BF16, name="z_tile", tag="z_tile", bufs=Z_BUFS)
                nc.sync.dma_start(out=z_tile[t][:], in_=z[t * P : (t + 1) * P, :])

        for first_two in range(2):
            load_g_rows(first_two)
            load_xz_again(first_two)

        def exponentials(t):
            inv_root[t] = early.tile([P, TOKENS], F32, name="inv_root", tag="inv_root")
            exp_v[t] = early.tile([P, TOKENS], F32, name="exp_v", tag="exp_v")
            exp_neg_v[t] = early.tile([P, TOKENS], F32, name="exp_neg_v", tag="exp_neg_v")
            for cols in pieces(t):
                nc.scalar.activation(
                    out=inv_root[t][:, cols], in_=log1p_sq[t][:, cols], func=ACT.Exp, scale=-0.5,
                    bias=ln_half_cz[:, t : t + 1],
                )
                nc.scalar.activation(
                    out=exp_v[t][:, cols], in_=asinh[t][:, cols], func=ACT.Exp,
                    scale=neg_two_zn[:, t : t + 1], bias=bias_v[:, t : t + 1],
                )
                nc.scalar.activation(
                    out=exp_neg_v[t][:, cols], in_=asinh[t][:, cols], func=ACT.Exp,
                    scale=two_zn[:, t : t + 1], bias=bias_neg_v[:, t : t + 1],
                )

        def to_token_layout(tiles, g):
            bank = psum.tile([P, PACK, P], F32, name="token_bank", tag="feed")
            for j in range(PACK):
                first = (g * PACK + j) * P
                for i, tile in enumerate(tiles):
                    nc.tensor.matmul(
                        out=bank[:, j, :], lhsT=tile[:, first : first + P], rhs=ident_f32[:], is_transpose=True,
                        start=(i == 0), stop=(i == len(tiles) - 1),
                    )
            return bank

        def start_gradients(t):
            batch, place = divmod(t, BATCH)
            u_xz[t] = late.tile([P, TOKENS], F32, name="u_xz", tag="u_xz", bufs=1)
            for g in range(PASSES):
                tokens = slice(g * K_PASS, (g + 1) * K_PASS)
                bank = xz_pass_to_o_layout(xz_again[t][:, g, :, :])
                nc.vector.tensor_tensor(out=u_xz[t][:, tokens], in0=inv_root[t][:, tokens], in1=bank[:], op=ALU.mult)
            load_xz_again(t + 2)
            if t > 0:
                sum_over_groups(t - 1)
            dv2[t] = late.tile([P, PASSES, PACK, P], F32, name="dv2", tag="dv2", bufs=1)
            for g in range(PASSES):
                bank = to_token_layout([exp_v[t], exp_neg_v[t]], g)
                nc.vector.tensor_tensor(
                    out=dv2[t][:, g, :, :], in0=g_rows[batch][:, g, :, place * P : (place + 1) * P], in1=bank[:], op=ALU.mult
                )
            if place == BATCH - 1:
                load_g_rows(batch + 2)

        def end_gradients(t):
            grouped[t] = late.tile([P, PASSES, P, PACK], BF16, name="grouped", tag="grouped", align_bytes=64)

            def times_u(g):
                bank = to_token_layout([inv_root[t]], g)
                nc.vector.tensor_tensor(
                    out=grouped[t][:, g, :, :].rearrange("p (c i) j -> p c j i", i=4),
                    in0=dv2[t][:, g, :, :].rearrange("p j (c i) -> p c j i", i=4),
                    in1=bank[:].rearrange("p j (c i) -> p c j i", i=4), op=ALU.mult,
                )

            def times_bracket(g):
                bank = to_token_layout([asinh[t], u_xz[t]], g)
                nc.vector.tensor_tensor(out=dv2[t][:, g, :, :], in0=dv2[t][:, g, :, :], in1=bank[:], op=ALU.mult)

            times_u(0)
            times_u(1)
            times_bracket(0)
            times_u(2)
            times_bracket(1)
            times_bracket(2)

        def sum_over_groups(t):
            sums[t] = psum.tile([P, P], F32, name="sums", tag="sums", bufs=1)
            blocks = [(g, j) for g in range(PASSES) for j in range(PACK)]
            for g, j in blocks:
                nc.tensor.matmul(
                    out=sums[t][:], lhsT=dv2[t][:, g, j, :], rhs=ident_f32[:], is_transpose=True,
                    start=((g, j) == blocks[0]), stop=((g, j) == blocks[-1]),
                )

        def sum_over_tokens(t):
            nc.vector.tensor_reduce(out=t_sum[:, t : t + 1], in_=sums[t][:], axis=mybir.AxisListType.X, op=ALU.add)

        def quantise_dxz(t):
            dxz_codes[t] = late.tile([P, PASSES, P], U32, name="dxz_codes", tag="dxz_codes", align_bytes=64)
            dxz_scales[t] = late.tile([P, PASSES, P], U8, name="dxz_scales", tag="dxz_scales", align_bytes=64)
            for g in range(PASSES):
                nc.vector.quantize_mx(
                    out=dxz_codes[t][:, g, :].bitcast(E5M2_X4),
                    scales=dxz_scales[t][:, g, :],
                    in_=grouped[t][:, g, :, :].rearrange("p o j -> p (o j)"),
                )

        def finish(t):
            nc.vector.tensor_scalar_mul(
                out=t_over_zn[:, t : t + 1], in0=t_sum[:, t : t + 1], scalar1=neg_inv_zn_sq[:, t : t + 1]
            )
            for n in range(D_HALVES):
                cols = slice(n * N_TILE, (n + 1) * N_TILE)
                product = psum.tile([P, N_TILE], F32, name="product", tag="product", bufs=2)
                for g in range(PASSES):
                    nc.tensor.matmul_mx(
                        out=product[:],
                        lhsT=dxz_codes[t][:, g, :].bitcast(E5M2_X4),
                        lhsT_scale=dxz_scales[t][:, g, :],
                        rhs=x_codes[:, g, cols].bitcast(E4M3_X4),
                        rhs_scale=x_scales[:, g, cols],
                        start=(g == 0),
                        stop=(g == PASSES - 1),
                    )
                result = late.tile([P, N_TILE], F32, name="result", tag="result", bufs=LATE_ROWS // 2)
                nc.vector.scalar_tensor_tensor(
                    out=result[:], in0=z_tile[t][:, cols], scalar=t_over_zn[:, t : t + 1], in1=product[:],
                    op0=ALU.mult, op1=ALU.add,
                )
                nc.sync.dma_start(out=out[t * P : (t + 1) * P, cols], in_=result[:])
            load_z_tile(t + Z_BUFS)

        def run(stage, t):
            if 0 <= t < O_TILES:
                stage(t)

        for k in range(BATCHES + 2):
            t = BATCH * k
            run(start_gradients, t - 2)
            run(finish, t - 4)
            if t - 3 == O_TILES - 1:
                sum_over_groups(O_TILES - 1)
            run(sum_over_tokens, t - 3)
            run(end_gradients, t - 2)
            if k > 0:
                run(second_log, t)
                run(second_log, t + 1)
            if k == 1:
                exponent_biases(next_tiles, nc.gpsimd)
                feature_quantities(other_tiles, nc.gpsimd)
            if k == 2:
                exponent_biases(other_tiles, nc.gpsimd)
            if k > 0:
                run(first_log, t + 2)
                run(first_log, t + 3)
            run(start_gradients, t - 1)
            run(shifted_xz, t + 4)
            run(shifted_xz, t + 5)
            run(quantise_dxz, t - 3)
            run(quantise_dxz, t - 2)
            run(sign, t + 4)
            run(sign, t + 5)
            run(absolute, t + 4)
            run(absolute, t + 5)
            run(exponentials, t)
            run(root, t + 2)
            run(root, t + 3)
            run(square, t + 4)
            run(finish, t - 3)
            run(sum_over_tokens, t - 2)
            run(end_gradients, t - 1)
            run(exponentials, t + 1)
            run(square, t + 5)
            if k == 0:
                for late_tile in range(4 * BATCH, O_TILES):
                    late_square_norm(late_tile)
                    load_late_rows(late_tile + LATE_ROWS)
                for first in range(Z_BUFS):
                    load_z_tile(first)
